import numpy as np
import ml_dtypes


def mxq(x, axis, fmt="e4m3"):
    dtype, down = {"e4m3": (ml_dtypes.float8_e4m3fn, 7), "e5m2": (ml_dtypes.float8_e5m2, 14)}[fmt]
    v = np.moveaxis(np.asarray(x, np.float32).astype(ml_dtypes.bfloat16).astype(np.float64), axis, -1)
    blocks = v.reshape(v.shape[:-1] + (-1, 32))
    amax = np.abs(blocks).max(-1, keepdims=True)
    byte = np.maximum(np.where(amax > 0, np.frexp(amax)[1] - 1 + 127, 0) - down, 1)
    scale = np.exp2(byte - 127.0)
    codes = (blocks / scale).astype(np.float32).astype(dtype).astype(np.float64)
    return np.moveaxis((codes * scale).reshape(v.shape), -1, axis)


WIDE = False


def mx_kscale(k):
    if not WIDE:
        return np.ones(k)
    levels = np.array([10, -10, 5, -5, 0])
    a = np.random.permutation(np.resize(levels, k // 512 * 4)).reshape(k // 512, 4)
    idx = np.arange(k)
    return np.exp2(a[idx // 512, idx % 128 // 32])


BF16 = ml_dtypes.bfloat16


def bf(x):
    return np.asarray(x, np.float32).astype(BF16)


def f64(x):
    return np.asarray(x).astype(np.float64)


B, HID, UD = 1024, 1024, 512


def sigmoid(v):
    return 1.0 / (1.0 + np.exp(-v))


def setup_inputs():
    s, t, u = mx_kscale(HID), mx_kscale(UD), mx_kscale(UD)
    return {
        "encoder_hidden": bf(np.random.standard_normal((B, HID)) * s),
        "spk_vectors": bf(np.random.standard_normal((B, UD)) * t),
        "adr_vectors": bf(np.random.standard_normal((B, UD)) * u),
        "WA_xp": bf(np.random.standard_normal((UD, HID)) / np.sqrt(HID) / s),
        "WA_hp": bf(np.random.standard_normal((UD, UD)) / np.sqrt(UD) / t),
        "VA_hp": bf(np.random.standard_normal((UD, UD)) / np.sqrt(UD) / u),
        "VA_hh": bf(np.random.standard_normal((UD, UD)) / np.sqrt(UD) / u),
    }


def reference(encoder_hidden, spk_vectors, adr_vectors, WA_xp, WA_hp, VA_hp, VA_hh):
    x, hs, ha = f64(encoder_hidden), f64(spk_vectors), f64(adr_vectors)
    p_t = sigmoid((mxq(x, 1, "e4m3") @ mxq(f64(WA_xp), 1, "e4m3").T)
                  + (mxq(hs, 1, "e4m3") @ mxq(f64(WA_hp), 1, "e4m3").T)
                  + (mxq(ha, 1, "e4m3") @ mxq(f64(VA_hp), 1, "e4m3").T))
    return mxq(p_t * ha, 1, "e4m3") @ mxq(f64(VA_hh), 1, "e4m3").T

@@ -1,0 +1,354 @@
+from contextlib import ExitStack
+
+import concourse.mybir as mybir
+from concourse.masks import make_identity
+
+F32 = mybir.dt.float32
+BF16 = mybir.dt.bfloat16
+U32 = mybir.dt.uint32
+U8 = mybir.dt.uint8
+FP8X4 = mybir.dt.float8_e4m3fn_x4
+SIGMOID = mybir.ActivationFunctionType.Sigmoid
+MULT = mybir.AluOpType.mult
+P = 128
+FLOPS = 2 * 1024 * 512 * (1024 + 512 + 512 + 512)
+
+STEPS = [
+    ("L", "Whp0"),
+    ("L", "Whp1"),
+    ("L", "hs0"),
+    ("L", "Vhp"),
+    ("L", "ha0"),
+    ("L", "x0"),
+    ("L", "Wx0"),
+    ("L", "Wx1"),
+    ("L", "Vhh"),
+    ("L", "hs1"),
+    ("L", "ha1"),
+    ("L", "x1"),
+    ("L", "hs2"),
+    ("L", "ha2"),
+    ("L", "x2"),
+    ("L", "hs3"),
+    ("L", "ha3"),
+    ("L", "x3"),
+    ("T", "Whp0", 4),
+    ("T", "Whp1", 5),
+    ("C", "Whp0", "S"),
+    ("T", "hs0", 6),
+    ("C", "Whp1", "S"),
+    ("Q", "Whp0"),
+    ("C", "hs0", "V"),
+    ("Q", "Whp1"),
+    ("T", "Vhp0", 7),
+    ("Q", "hs0"),
+    ("T", "Vhp1", 4),
+    ("C", "Vhp0", "V"),
+    ("T", "ha0", 5),
+    ("C", "Vhp1", "S"),
+    ("MA", 0),
+    ("Q", "Vhp0"),
+    ("C", "ha0", "S"),
+    ("Q", "Vhp1"),
+    ("T", "x0k0", 6),
+    ("Q", "ha0"),
+    ("T", "x0k1", 7),
+    ("C", "x0k0", "V"),
+    ("MA", 1),
+    ("C", "x0k1", "V"),
+    ("T", "Wx0k0", 4),
+    ("Q", "x0k0"),
+    ("Q", "x0k1"),
+    ("T", "Wx0k1", 5),
+    ("C", "Wx0k0", "V"),
+    ("T", "Wx1k0", 6),
+    ("C", "Wx0k1", "S"),
+    ("T", "Wx1k1", 7),
+    ("Q", "Wx0k0"),
+    ("C", "Wx1k0", "V"),
+    ("T", "Vhh0", 4),
+    ("T", "Vhh1", 5),
+    ("Q", "Wx0k1"),
+    ("T", "hs1", 6),
+    ("Q", "Wx1k0"),
+    ("C", "Vhh1", "S"),
+    ("C", "Wx1k1", "V"),
+    ("MA", 2),
+    ("C", "Vhh0", "V"),
+    ("T", "ha1", 7),
+    ("SA", 0),
+    ("Q", "Wx1k1"),
+    ("SA", 1),
+    ("T", "x1k0", 4),
+    ("Q", "Vhh0"),
+    ("Q", "Vhh1"),
+    ("T", "x1k1", 5),
+    ("C", "hs1", "V"),
+    ("C", "x1k0", "S"),
+    ("MA", 3),
+    ("C", "ha1", "V"),
+    ("C", "x1k1", "S"),
+    ("T", "hs2", 6),
+    ("Q", "hs1"),
+    ("SA", 2),
+    ("T", "ha2", 7),
+    ("Q", "ha1"),
+    ("C", "hs2", "S"),
+    ("Q", "x1k0"),
+    ("T", "x2k0", 4),
+    ("Q", "x1k1"),
+    ("SA", 3),
+    ("T", "x2k1", 5),
+    ("Q", "hs2"),
+    ("C", "x2k0", "S"),
+    ("T", "hs3", 6),
+    ("C", "ha2", "V"),
+    ("MB", 1, 0),
+    ("C", "hs3", "S"),
+    ("Q", "x2k0"),
+    ("Q", "ha2"),
+    ("C", "x2k1", "V"),
+    ("MB", 1, 1),
+    ("SB", 1, 0),
+    ("Q", "hs3"),
+    ("Q", "x2k1"),
+    ("PR", 0, 1),
+    ("T", "ha3", 7),
+    ("SB", 1, 1),
+    ("T", "x3k0", 4),
+    ("QG", 0, 1),
+    ("PR", 1, 1),
+    ("T", "x3k1", 5),
+    ("C", "ha3", "S"),
+    ("S2", 0, 2),
+    ("QG", 1, 1),
+    ("C", "x3k0", "S"),
+    ("MB", 2, 0),
+    ("Q", "ha3"),
+    ("C", "x3k1", "S"),
+    ("Q", "x3k0"),
+    ("OC", 0, "S"),
+    ("S2", 1, 3),
+    ("Q", "x3k1"),
+    ("MB", 2, 1),
+    ("SB", 2, 0),
+    ("OC", 1, "V"),
+    ("PR", 2, 1),
+    ("ST", 0, 2),
+    ("MB", 3, 0),
+    ("SB", 2, 1),
+    ("QG", 2, 1),
+    ("PR", 3, 1),
+    ("S2", 2, 2),
+    ("QG", 3, 1),
+    ("PR", 4, 1),
+    ("MB", 3, 1),
+    ("SB", 3, 0),
+    ("OC", 2, "S"),
+    ("QG", 4, 1),
+    ("PR", 5, 1),
+    ("S2", 3, 3),
+    ("S2", 4, 2),
+    ("SB", 3, 1),
+    ("QG", 5, 1),
+    ("OC", 3, "V"),
+    ("OC", 4, "S"),
+    ("PR", 6, 1),
+    ("ST", 2, 2),
+    ("S2", 5, 3),
+    ("QG", 6, 1),
+    ("OC", 5, "S"),
+    ("PR", 7, 1),
+    ("S2", 6, 2),
+    ("ST", 4, 2),
+    ("QG", 7, 1),
+    ("OC", 6, "S"),
+    ("S2", 7, 3),
+    ("OC", 7, "S"),
+    ("ST", 6, 1),
+    ("ST", 7, 1),
+]
+
+
+def tile_updatespeaker_pa_kernel(
+    tc, encoder_hidden, spk_vectors, adr_vectors, WA_xp, WA_hp, VA_hp, VA_hh, out
+):
+    nc = tc.nc
+    with ExitStack() as ctx:
+        keep = ctx.enter_context(tc.tile_pool(name="keep", bufs=1))
+        psum = ctx.enter_context(tc.psum_pool(name="psum", bufs=1))
+
+        ident = keep.tile([P, P], F32, name="ident")
+        warm_in = keep.tile([P, 1], F32, name="warm_in")
+        warm_out = keep.tile([P, 1], F32, name="warm_out")
+
+        whp_raw = keep.tile([P, 4, 512], BF16, name="whp_raw")
+        vhp_raw = keep.tile([P, 4, 512], BF16, name="vhp_raw")
+        vhh_raw = keep.tile([P, 4, 512], BF16, name="vhh_raw")
+        wxp_raw = keep.tile([P, 4, 1024], BF16, name="wxp_raw")
+        hs_raw = keep.tile([P, 8, 512], BF16, name="hs_raw")
+        ha_raw = keep.tile([P, 8, 512], BF16, name="ha_raw")
+        x_raw = keep.tile([P, 8, 1024], BF16, name="x_raw")
+
+        w_grp = [keep.tile([P, 512, 2], F32, name="w_grp%d" % s, align_bytes=64) for s in range(5)]
+        w_codes = [keep.tile([P, 512], U32, name="w_codes%d" % s, align_bytes=64) for s in range(5)]
+        w_scl = [keep.tile([P, 512], U8, name="w_scl%d" % s, align_bytes=64) for s in range(5)]
+        a_grp = [keep.tile([P, 1024, 2], F32, name="a_grp%d" % s, align_bytes=64) for s in range(4)]
+        a_codes = [keep.tile([P, 1024], U32, name="a_codes%d" % s, align_bytes=64) for s in range(4)]
+        a_scl = [keep.tile([P, 1024], U8, name="a_scl%d" % s, align_bytes=64) for s in range(4)]
+        sig = keep.tile([P, 4, 1024], F32, name="sig")
+        g_grp = keep.tile([P, 1024, 4], BF16, name="g_grp", align_bytes=64)
+        g_codes = keep.tile([P, 1024], U32, name="g_codes", align_bytes=64)
+        g_scl = keep.tile([P, 1024], U8, name="g_scl", align_bytes=64)
+        o_sb = keep.tile([P, 8, 512], F32, name="o_sb")
+
+        def w_rows(w):
+            return w.rearrange("(u p e) k -> p u e k", u=2, e=2)
+
+        def a_rows(a):
+            return a.rearrange("(p r) k -> p r k", r=8)
+
+        loads = {
+            "Whp0": (whp_raw[:, 0:2, :], w_rows(WA_hp)[:, 0, :, :]),
+            "Whp1": (whp_raw[:, 2:4, :], w_rows(WA_hp)[:, 1, :, :]),
+            "Vhp": (vhp_raw[:].rearrange("p (u e) k -> p u e k", u=2), w_rows(VA_hp)),
+            "Wx0": (wxp_raw[:, 0:2, :], w_rows(WA_xp)[:, 0, :, :]),
+            "Wx1": (wxp_raw[:, 2:4, :], w_rows(WA_xp)[:, 1, :, :]),
+            "Vhh": (vhh_raw[:], VA_hh.rearrange("(j p) k -> p j k", p=P)),
+        }
+        for j in range(4):
+            loads["hs%d" % j] = (hs_raw[:, 2 * j : 2 * j + 2, :], a_rows(spk_vectors)[:, 2 * j : 2 * j + 2, :])
+            loads["ha%d" % j] = (ha_raw[:, 2 * j : 2 * j + 2, :], a_rows(adr_vectors)[:, 2 * j : 2 * j + 2, :])
+            loads["x%d" % j] = (x_raw[:, 2 * j : 2 * j + 2, :], a_rows(encoder_hidden)[:, 2 * j : 2 * j + 2, :])
+
+        units = {}
+        for h in range(2):
+            units["Whp%d" % h] = (whp_raw, 2 * h, 0, w_grp[0], w_codes[0], w_scl[0], 256 * h)
+            units["Vhp%d" % h] = (vhp_raw, 2 * h, 0, w_grp[1], w_codes[1], w_scl[1], 256 * h)
+            units["Vhh%d" % h] = (vhh_raw, 2 * h, 0, w_grp[4], w_codes[4], w_scl[4], 256 * h)
+            for g in range(2):
+                units["Wx%dk%d" % (h, g)] = (wxp_raw, 2 * h, 256 * g, w_grp[2 + g], w_codes[2 + g], w_scl[2 + g], 256 * h)
+        for j in range(4):
+            units["hs%d" % j] = (hs_raw, 2 * j, 0, a_grp[0], a_codes[0], a_scl[0], 256 * j)
+            units["ha%d" % j] = (ha_raw, 2 * j, 0, a_grp[1], a_codes[1], a_scl[1], 256 * j)
+            for g in range(2):
+                units["x%dk%d" % (j, g)] = (x_raw, 2 * j, 256 * g, a_grp[2 + g], a_codes[2 + g], a_scl[2 + g], 256 * j)
+
+        live = {}
+
+        def bank(i, shape, label):
+            return psum.tile(shape, F32, tag="bank%d" % i, name=label)
+
+        def mx(dst, s, t, c0, n, start, stop):
+            nc.tensor.matmul_mx(
+                out=dst,
+                lhsT=w_codes[s][:, 128 * t : 128 * t + 128].bitcast(FP8X4),
+                lhsT_scale=w_scl[s][:, 128 * t : 128 * t + 128],
+                rhs=a_codes[s][:, c0 : c0 + n].bitcast(FP8X4),
+                rhs_scale=a_scl[s][:, c0 : c0 + n],
+                start=start,
+                stop=stop,
+            )
+
+        nc.vector.memset(warm_in[:], 0.0)
+        make_identity(nc, ident[:])
+        nc.scalar.activation(out=warm_out[:], in_=warm_in[:], func=SIGMOID)
+
+        for st in STEPS:
+            kind = st[0]
+            if kind == "L":
+                nc.sync.dma_start(out=loads[st[1]][0], in_=loads[st[1]][1])
+            elif kind == "T":
+                raw, row, w0, grp, codes, scl, c0 = units[st[1]]
+                bk = bank(st[2], [P, 2, 256], "tp_" + st[1])
+                words = raw[:].bitcast(F32)
+                for half in range(2):
+                    for i in range(2):
+                        nc.tensor.transpose(
+                            bk[:, half, 128 * i : 128 * i + 128],
+                            words[:, row + i, w0 + 128 * half : w0 + 128 * half + 128],
+                            ident[:],
+                        )
+                live[st[1]] = bk
+            elif kind == "C":
+                raw, row, w0, grp, codes, scl, c0 = units[st[1]]
+                src = live[st[1]][:].rearrange("p u c -> p c u")
+                if st[2] == "V":
+                    nc.vector.tensor_copy(out=grp[:, c0 : c0 + 256, :], in_=src)
+                else:
+                    nc.scalar.copy(out=grp[:, c0 : c0 + 256, :], in_=src)
+            elif kind == "Q":
+                raw, row, w0, grp, codes, scl, c0 = units[st[1]]
+                nc.vector.quantize_mx(
+                    out=codes[:, c0 : c0 + 256].bitcast(FP8X4),
+                    scales=scl[:, c0 : c0 + 256],
+                    in_=grp[:].bitcast(BF16)[:, c0 : c0 + 256, :].rearrange("p c t -> p (c t)"),
+                )
+            elif kind == "MA":
+                s = st[1]
+                if s == 0:
+                    for t in range(4):
+                        live["gate0_%d" % t] = bank(t, [P, 256], "gate0_%d" % t)
+                if s < 2:
+                    for t in range(4):
+                        mx(live["gate0_%d" % t][:], s, t, 0, 256, s == 0, False)
+                else:
+                    for t in (2 * s - 4, 2 * s - 3):
+                        mx(live["gate0_%d" % t][:], 2, t, 0, 256, False, False)
+                        mx(live["gate0_%d" % t][:], 3, t, 0, 256, False, True)
+            elif kind == "SA":
+                t = st[1]
+                nc.scalar.activation(out=sig[:, t, 0:256], in_=live["gate0_%d" % t][:], func=SIGMOID)
+            elif kind == "MB":
+                j, h = st[1], st[2]
+                bk = bank(h, [P, 2, 256], "gate%d_%d" % (j, h))
+                for i in range(2):
+                    for s in range(4):
+                        mx(bk[:, i, :], s, 2 * h + i, 256 * j, 256, s == 0, s == 3)
+                live["gate%d_%d" % (j, h)] = bk
+            elif kind == "SB":
+                j, h = st[1], st[2]
+                nc.scalar.activation(
+                    out=sig[:, 2 * h : 2 * h + 2, 256 * j : 256 * j + 256],
+                    in_=live["gate%d_%d" % (j, h)][:],
+                    func=SIGMOID,
+                )
+            elif kind == "PR":
+                c0, n = 128 * st[1], 128 * st[2]
+                nc.vector.tensor_tensor(
+                    out=g_grp[:, c0 : c0 + n, :],
+                    in0=sig[:, :, c0 : c0 + n].rearrange("p t b -> p b t"),
+                    in1=a_grp[1][:].bitcast(BF16)[:, c0 : c0 + n, :],
+                    op=MULT,
+                )
+            elif kind == "QG":
+                c0, n = 128 * st[1], 128 * st[2]
+                nc.vector.quantize_mx(
+                    out=g_codes[:, c0 : c0 + n].bitcast(FP8X4),
+                    scales=g_scl[:, c0 : c0 + n],
+                    in_=g_grp[:, c0 : c0 + n, :].rearrange("p c t -> p (c t)"),
+                )
+            elif kind == "S2":
+                r = st[1]
+                bk = bank(st[2], [P, 512], "out_%d" % r)
+                nc.tensor.matmul_mx(
+                    out=bk[:],
+                    lhsT=g_codes[:, 128 * r : 128 * r + 128].bitcast(FP8X4),
+                    lhsT_scale=g_scl[:, 128 * r : 128 * r + 128],
+                    rhs=w_codes[4][:].bitcast(FP8X4),
+                    rhs_scale=w_scl[4][:],
+                    start=True,
+                    stop=True,
+                )
+                live["out_%d" % r] = bk
+            elif kind == "OC":
+                r = st[1]
+                if st[2] == "V":
+                    nc.vector.tensor_copy(out=o_sb[:, r, :], in_=live["out_%d" % r][:])
+                else:
+                    nc.scalar.copy(out=o_sb[:, r, :], in_=live["out_%d" % r][:])
+            elif kind == "ST":
+                r0, n = st[1], st[2]
+                nc.sync.dma_start(
+                    out=out.rearrange("(p r) o -> p r o", r=8)[:, r0 : r0 + n, :], in_=o_sb[:, r0 : r0 + n, :]
+                )

@@ -177,6 +177,7 @@ def tile_updatespeaker_pa_kernel(
     with ExitStack() as ctx:
         keep = ctx.enter_context(tc.tile_pool(name="keep", bufs=1))
         psum = ctx.enter_context(tc.psum_pool(name="psum", bufs=1))
+        ctx.enter_context(tc.manual_schedule())
 
         ident = keep.tile([P, P], F32, name="ident")
         warm_in = keep.tile([P, 1], F32, name="warm_in")

@@ -31,21 +31,22 @@ STEPS = [
     ("L", "x2"),
     ("L", "hs3"),
     ("L", "ha3"),
-    ("L", "x3"),
+    ("L", "x6s"),
+    ("L", "x7s"),
     ("T", "Whp0", 4),
     ("T", "Whp1", 5),
     ("C", "Whp0", "S"),
     ("T", "hs0", 6),
-    ("C", "Whp1", "S"),
+    ("C", "Whp1", "V"),
     ("Q", "Whp0"),
-    ("C", "hs0", "V"),
+    ("C", "hs0", "S"),
     ("Q", "Whp1"),
     ("T", "Vhp0", 7),
     ("Q", "hs0"),
     ("T", "Vhp1", 4),
-    ("C", "Vhp0", "V"),
+    ("C", "Vhp0", "S"),
     ("T", "ha0", 5),
-    ("C", "Vhp1", "S"),
+    ("C", "Vhp1", "V"),
     ("MA", 0),
     ("Q", "Vhp0"),
     ("C", "ha0", "S"),
@@ -53,118 +54,118 @@ STEPS = [
     ("T", "x0k0", 6),
     ("Q", "ha0"),
     ("T", "x0k1", 7),
-    ("C", "x0k0", "V"),
-    ("MA", 1),
-    ("C", "x0k1", "V"),
+    ("C", "x0k0", "S"),
     ("T", "Wx0k0", 4),
-    ("Q", "x0k0"),
-    ("Q", "x0k1"),
+    ("C", "x0k1", "V"),
     ("T", "Wx0k1", 5),
-    ("C", "Wx0k0", "V"),
+    ("Q", "x0k0"),
+    ("C", "Wx0k0", "S"),
+    ("Q", "x0k1"),
     ("T", "Wx1k0", 6),
-    ("C", "Wx0k1", "S"),
+    ("C", "Wx0k1", "V"),
     ("T", "Wx1k1", 7),
     ("Q", "Wx0k0"),
-    ("C", "Wx1k0", "V"),
-    ("T", "Vhh0", 4),
-    ("T", "Vhh1", 5),
+    ("C", "Wx1k0", "S"),
     ("Q", "Wx0k1"),
-    ("T", "hs1", 6),
+    ("T", "Vhh0", 4),
+    ("C", "Wx1k1", "S"),
     ("Q", "Wx1k0"),
-    ("C", "Vhh1", "S"),
-    ("C", "Wx1k1", "V"),
-    ("MA", 2),
-    ("C", "Vhh0", "V"),
-    ("T", "ha1", 7),
-    ("SA", 0),
+    ("T", "Vhh1", 5),
+    ("C", "Vhh0", "S"),
     ("Q", "Wx1k1"),
-    ("SA", 1),
-    ("T", "x1k0", 4),
+    ("MA", 1),
+    ("C", "Vhh1", "V"),
+    ("T", "hs1", 6),
     ("Q", "Vhh0"),
     ("Q", "Vhh1"),
-    ("T", "x1k1", 5),
-    ("C", "hs1", "V"),
-    ("C", "x1k0", "S"),
+    ("MA", 2),
+    ("C", "hs1", "S"),
     ("MA", 3),
-    ("C", "ha1", "V"),
-    ("C", "x1k1", "S"),
-    ("T", "hs2", 6),
+    ("SA", 0),
     ("Q", "hs1"),
+    ("T", "ha1", 7),
+    ("SA", 1),
     ("SA", 2),
+    ("T", "x1k0", 4),
+    ("SA", 3),
+    ("C", "ha1", "S"),
+    ("PR", 0, 1),
+    ("T", "x1k1", 5),
+    ("C", "x1k0", "S"),
+    ("PR", 1, 1),
+    ("T", "hs2", 6),
+    ("C", "x1k1", "S"),
+    ("QG", 0, 1),
     ("T", "ha2", 7),
+    ("QG", 1, 1),
     ("Q", "ha1"),
     ("C", "hs2", "S"),
     ("Q", "x1k0"),
     ("T", "x2k0", 4),
     ("Q", "x1k1"),
-    ("SA", 3),
-    ("T", "x2k1", 5),
+    ("C", "ha2", "S"),
     ("Q", "hs2"),
+    ("T", "x2k1", 5),
     ("C", "x2k0", "S"),
-    ("T", "hs3", 6),
-    ("C", "ha2", "V"),
-    ("MB", 1, 0),
-    ("C", "hs3", "S"),
-    ("Q", "x2k0"),
     ("Q", "ha2"),
-    ("C", "x2k1", "V"),
+    ("T", "hs3", 6),
+    ("C", "x2k1", "S"),
+    ("Q", "x2k0"),
+    ("T", "ha3", 7),
+    ("C", "hs3", "S"),
+    ("Q", "x2k1"),
+    ("TX", 6, 4),
+    ("C", "ha3", "S"),
+    ("Q", "hs3"),
+    ("TX", 7, 5),
+    ("CX", 6, "S"),
+    ("Q", "ha3"),
+    ("S2", 0, 2),
+    ("S2", 1, 3),
+    ("CX", 7, "S"),
+    ("QX", 6),
+    ("MB", 1, 0),
+    ("OC", 0, "S"),
+    ("OC", 1, "V"),
+    ("QX", 7),
+    ("ST", 0, 2),
     ("MB", 1, 1),
     ("SB", 1, 0),
-    ("Q", "hs3"),
-    ("Q", "x2k1"),
-    ("PR", 0, 1),
-    ("T", "ha3", 7),
-    ("SB", 1, 1),
-    ("T", "x3k0", 4),
-    ("QG", 0, 1),
-    ("PR", 1, 1),
-    ("T", "x3k1", 5),
-    ("C", "ha3", "S"),
-    ("S2", 0, 2),
-    ("QG", 1, 1),
-    ("C", "x3k0", "S"),
     ("MB", 2, 0),
-    ("Q", "ha3"),
-    ("C", "x3k1", "S"),
-    ("Q", "x3k0"),
-    ("OC", 0, "S"),
-    ("S2", 1, 3),
-    ("Q", "x3k1"),
+    ("SB", 1, 1),
+    ("PR", 2, 1),
     ("MB", 2, 1),
     ("SB", 2, 0),
-    ("OC", 1, "V"),
-    ("PR", 2, 1),
-    ("ST", 0, 2),
-    ("MB", 3, 0),
-    ("SB", 2, 1),
-    ("QG", 2, 1),
     ("PR", 3, 1),
-    ("S2", 2, 2),
+    ("QG", 2, 1),
+    ("MD", 6, 0),
     ("QG", 3, 1),
+    ("SB", 2, 1),
     ("PR", 4, 1),
-    ("MB", 3, 1),
-    ("SB", 3, 0),
-    ("OC", 2, "S"),
-    ("QG", 4, 1),
-    ("PR", 5, 1),
+    ("S2", 2, 2),
     ("S2", 3, 3),
-    ("S2", 4, 2),
-    ("SB", 3, 1),
-    ("QG", 5, 1),
+    ("SD", 6),
+    ("PR", 5, 1),
+    ("MD", 7, 1),
+    ("OC", 2, "S"),
     ("OC", 3, "V"),
-    ("OC", 4, "S"),
-    ("PR", 6, 1),
+    ("QG", 4, 1),
     ("ST", 2, 2),
+    ("QG", 5, 1),
+    ("PR", 6, 1),
+    ("S2", 4, 2),
+    ("SD", 7),
     ("S2", 5, 3),
     ("QG", 6, 1),
-    ("OC", 5, "S"),
+    ("OC", 4, "S"),
     ("PR", 7, 1),
     ("S2", 6, 2),
-    ("ST", 4, 2),
-    ("QG", 7, 1),
+    ("OC", 5, "V"),
     ("OC", 6, "S"),
+    ("QG", 7, 1),
+    ("ST", 4, 2),
     ("S2", 7, 3),
-    ("OC", 7, "S"),
+    ("OC", 7, "V"),
     ("ST", 6, 1),
     ("ST", 7, 1),
 ]
@@ -177,7 +178,6 @@ def tile_updatespeaker_pa_kernel(
     with ExitStack() as ctx:
         keep = ctx.enter_context(tc.tile_pool(name="keep", bufs=1))
         psum = ctx.enter_context(tc.psum_pool(name="psum", bufs=1))
-        ctx.enter_context(tc.manual_schedule())
 
         ident = keep.tile([P, P], F32, name="ident")
         warm_in = keep.tile([P, 1], F32, name="warm_in")
@@ -191,12 +191,12 @@ def tile_updatespeaker_pa_kernel(
         ha_raw = keep.tile([P, 8, 512], BF16, name="ha_raw")
         x_raw = keep.tile([P, 8, 1024], BF16, name="x_raw")
 
-        w_grp = [keep.tile([P, 512, 2], F32, name="w_grp%d" % s, align_bytes=64) for s in range(5)]
-        w_codes = [keep.tile([P, 512], U32, name="w_codes%d" % s, align_bytes=64) for s in range(5)]
-        w_scl = [keep.tile([P, 512], U8, name="w_scl%d" % s, align_bytes=64) for s in range(5)]
-        a_grp = [keep.tile([P, 1024, 2], F32, name="a_grp%d" % s, align_bytes=64) for s in range(4)]
-        a_codes = [keep.tile([P, 1024], U32, name="a_codes%d" % s, align_bytes=64) for s in range(4)]
-        a_scl = [keep.tile([P, 1024], U8, name="a_scl%d" % s, align_bytes=64) for s in range(4)]
+        w_grp = keep.tile([P, 5, 512, 2], F32, name="w_grp", align_bytes=64)
+        w_codes = keep.tile([P, 5, 512], U32, name="w_codes", align_bytes=64)
+        w_scl = keep.tile([P, 5, 512], U8, name="w_scl", align_bytes=64)
+        a_grp = keep.tile([P, 4, 1024, 2], F32, name="a_grp", align_bytes=64)
+        a_codes = keep.tile([P, 4, 1024], U32, name="a_codes", align_bytes=64)
+        a_scl = keep.tile([P, 4, 1024], U8, name="a_scl", align_bytes=64)
         sig = keep.tile([P, 4, 1024], F32, name="sig")
         g_grp = keep.tile([P, 1024, 4], BF16, name="g_grp", align_bytes=64)
         g_codes = keep.tile([P, 1024], U32, name="g_codes", align_bytes=64)
@@ -221,19 +221,21 @@ def tile_updatespeaker_pa_kernel(
             loads["hs%d" % j] = (hs_raw[:, 2 * j : 2 * j + 2, :], a_rows(spk_vectors)[:, 2 * j : 2 * j + 2, :])
             loads["ha%d" % j] = (ha_raw[:, 2 * j : 2 * j + 2, :], a_rows(adr_vectors)[:, 2 * j : 2 * j + 2, :])
             loads["x%d" % j] = (x_raw[:, 2 * j : 2 * j + 2, :], a_rows(encoder_hidden)[:, 2 * j : 2 * j + 2, :])
+        for r in range(8):
+            loads["x%ds" % r] = (x_raw[:, r : r + 1, :], a_rows(encoder_hidden)[:, r : r + 1, :])
 
         units = {}
         for h in range(2):
-            units["Whp%d" % h] = (whp_raw, 2 * h, 0, w_grp[0], w_codes[0], w_scl[0], 256 * h)
-            units["Vhp%d" % h] = (vhp_raw, 2 * h, 0, w_grp[1], w_codes[1], w_scl[1], 256 * h)
-            units["Vhh%d" % h] = (vhh_raw, 2 * h, 0, w_grp[4], w_codes[4], w_scl[4], 256 * h)
+            units["Whp%d" % h] = (whp_raw, 2 * h, 0, w_grp, w_codes, w_scl, 0, 256 * h)
+            units["Vhp%d" % h] = (vhp_raw, 2 * h, 0, w_grp, w_codes, w_scl, 1, 256 * h)
+            units["Vhh%d" % h] = (vhh_raw, 2 * h, 0, w_grp, w_codes, w_scl, 4, 256 * h)
             for g in range(2):
-                units["Wx%dk%d" % (h, g)] = (wxp_raw, 2 * h, 256 * g, w_grp[2 + g], w_codes[2 + g], w_scl[2 + g], 256 * h)
+                units["Wx%dk%d" % (h, g)] = (wxp_raw, 2 * h, 256 * g, w_grp, w_codes, w_scl, 2 + g, 256 * h)
         for j in range(4):
-            units["hs%d" % j] = (hs_raw, 2 * j, 0, a_grp[0], a_codes[0], a_scl[0], 256 * j)
-            units["ha%d" % j] = (ha_raw, 2 * j, 0, a_grp[1], a_codes[1], a_scl[1], 256 * j)
+            units["hs%d" % j] = (hs_raw, 2 * j, 0, a_grp, a_codes, a_scl, 0, 256 * j)
+            units["ha%d" % j] = (ha_raw, 2 * j, 0, a_grp, a_codes, a_scl, 1, 256 * j)
             for g in range(2):
-                units["x%dk%d" % (j, g)] = (x_raw, 2 * j, 256 * g, a_grp[2 + g], a_codes[2 + g], a_scl[2 + g], 256 * j)
+                units["x%dk%d" % (j, g)] = (x_raw, 2 * j, 256 * g, a_grp, a_codes, a_scl, 2 + g, 256 * j)
 
         live = {}
 
@@ -243,13 +245,19 @@ def tile_updatespeaker_pa_kernel(
         def mx(dst, s, t, c0, n, start, stop):
             nc.tensor.matmul_mx(
                 out=dst,
-                lhsT=w_codes[s][:, 128 * t : 128 * t + 128].bitcast(FP8X4),
-                lhsT_scale=w_scl[s][:, 128 * t : 128 * t + 128],
-                rhs=a_codes[s][:, c0 : c0 + n].bitcast(FP8X4),
-                rhs_scale=a_scl[s][:, c0 : c0 + n],
+                lhsT=w_codes[:, s, 128 * t : 128 * t + 128].bitcast(FP8X4),
+                lhsT_scale=w_scl[:, s, 128 * t : 128 * t + 128],
+                rhs=a_codes[:, s, c0 : c0 + n].bitcast(FP8X4),
+                rhs_scale=a_scl[:, s, c0 : c0 + n],
                 start=start,
                 stop=stop,
             )
+
+        def copy_out(eng, dst, src):
+            if eng == "V":
+                nc.vector.tensor_copy(out=dst, in_=src)
+            else:
+                nc.scalar.copy(out=dst, in_=src)
 
         nc.vector.memset(warm_in[:], 0.0)
         make_identity(nc, ident[:])
@@ -260,7 +268,7 @@ def tile_updatespeaker_pa_kernel(
             if kind == "L":
                 nc.sync.dma_start(out=loads[st[1]][0], in_=loads[st[1]][1])
             elif kind == "T":
-                raw, row, w0, grp, codes, scl, c0 = units[st[1]]
+                raw, row, w0, grp, codes, scl, s, c0 = units[st[1]]
                 bk = bank(st[2], [P, 2, 256], "tp_" + st[1])
                 words = raw[:].bitcast(F32)
                 for half in range(2):
@@ -272,19 +280,39 @@ def tile_updatespeaker_pa_kernel(
                         )
                 live[st[1]] = bk
             elif kind == "C":
-                raw, row, w0, grp, codes, scl, c0 = units[st[1]]
-                src = live[st[1]][:].rearrange("p u c -> p c u")
-                if st[2] == "V":
-                    nc.vector.tensor_copy(out=grp[:, c0 : c0 + 256, :], in_=src)
-                else:
-                    nc.scalar.copy(out=grp[:, c0 : c0 + 256, :], in_=src)
+                raw, row, w0, grp, codes, scl, s, c0 = units[st[1]]
+                copy_out(st[2], grp[:, s, c0 : c0 + 256, :], live[st[1]][:].rearrange("p u c -> p c u"))
             elif kind == "Q":
-                raw, row, w0, grp, codes, scl, c0 = units[st[1]]
+                raw, row, w0, grp, codes, scl, s, c0 = units[st[1]]
                 nc.vector.quantize_mx(
-                    out=codes[:, c0 : c0 + 256].bitcast(FP8X4),
-                    scales=scl[:, c0 : c0 + 256],
-                    in_=grp[:].bitcast(BF16)[:, c0 : c0 + 256, :].rearrange("p c t -> p (c t)"),
+                    out=codes[:, s, c0 : c0 + 256].bitcast(FP8X4),
+                    scales=scl[:, s, c0 : c0 + 256],
+                    in_=grp[:].bitcast(BF16)[:, s, c0 : c0 + 256, :].rearrange("p c t -> p (c t)"),
                 )
+            elif kind == "TX":
+                r = st[1]
+                bk = bank(st[2], [P, 2, 2, 128], "tpx_%d" % r)
+                words = x_raw[:].bitcast(F32)
+                for g in range(2):
+                    for half in range(2):
+                        w0 = 256 * g + 128 * half
+                        nc.tensor.transpose(bk[:, g, half, :], words[:, r, w0 : w0 + 128], ident[:])
+                live["x%ds" % r] = bk
+            elif kind == "CX":
+                r = st[1]
+                copy_out(
+                    st[2],
+                    a_grp[:, 2:4, 128 * r : 128 * r + 128, :],
+                    live["x%ds" % r][:].rearrange("p g u c -> p g c u"),
+                )
+            elif kind == "QX":
+                r = st[1]
+                for s in (2, 3):
+                    nc.vector.quantize_mx(
+                        out=a_codes[:, s, 128 * r : 128 * r + 128].bitcast(FP8X4),
+                        scales=a_scl[:, s, 128 * r : 128 * r + 128],
+                        in_=a_grp[:].bitcast(BF16)[:, s, 128 * r : 128 * r + 128, :].rearrange("p c t -> p (c t)"),
+                    )
             elif kind == "MA":
                 s = st[1]
                 if s == 0:
@@ -314,12 +342,24 @@ def tile_updatespeaker_pa_kernel(
                     in_=live["gate%d_%d" % (j, h)][:],
                     func=SIGMOID,
                 )
+            elif kind == "MD":
+                r = st[1]
+                bk = bank(st[2], [P, 4, 128], "gater_%d" % r)
+                for t in range(4):
+                    for s in range(4):
+                        mx(bk[:, t, :], s, t, 128 * r, 128, s == 0, s == 3)
+                live["gater_%d" % r] = bk
+            elif kind == "SD":
+                r = st[1]
+                nc.scalar.activation(
+                    out=sig[:, :, 128 * r : 128 * r + 128], in_=live["gater_%d" % r][:], func=SIGMOID
+                )
             elif kind == "PR":
                 c0, n = 128 * st[1], 128 * st[2]
                 nc.vector.tensor_tensor(
                     out=g_grp[:, c0 : c0 + n, :],
                     in0=sig[:, :, c0 : c0 + n].rearrange("p t b -> p b t"),
-                    in1=a_grp[1][:].bitcast(BF16)[:, c0 : c0 + n, :],
+                    in1=a_grp[:].bitcast(BF16)[:, 1, c0 : c0 + n, :],
                     op=MULT,
                 )
             elif kind == "QG":
@@ -336,18 +376,15 @@ def tile_updatespeaker_pa_kernel(
                     out=bk[:],
                     lhsT=g_codes[:, 128 * r : 128 * r + 128].bitcast(FP8X4),
                     lhsT_scale=g_scl[:, 128 * r : 128 * r + 128],
-                    rhs=w_codes[4][:].bitcast(FP8X4),
-                    rhs_scale=w_scl[4][:],
+                    rhs=w_codes[:, 4, :].bitcast(FP8X4),
+                    rhs_scale=w_scl[:, 4, :],
                     start=True,
                     stop=True,
                 )
                 live["out_%d" % r] = bk
             elif kind == "OC":
                 r = st[1]
-                if st[2] == "V":
-                    nc.vector.tensor_copy(out=o_sb[:, r, :], in_=live["out_%d" % r][:])
-                else:
-                    nc.scalar.copy(out=o_sb[:, r, :], in_=live["out_%d" % r][:])
+                copy_out(st[2], o_sb[:, r, :], live["out_%d" % r][:])
             elif kind == "ST":
                 r0, n = st[1], st[2]
                 nc.sync.dma_start(

@@ -31,141 +31,141 @@ STEPS = [
     ("L", "x2"),
     ("L", "hs3"),
     ("L", "ha3"),
-    ("L", "x6s"),
-    ("L", "x7s"),
-    ("T", "Whp0", 4),
-    ("T", "Whp1", 5),
+    ("L", "x3"),
+    ("W", 7, 4),
+    ("T", "Whp0", 4, 1),
+    ("T", "Whp1", 5, 1),
     ("C", "Whp0", "S"),
-    ("T", "hs0", 6),
-    ("C", "Whp1", "V"),
+    ("T", "hs0", 6, 1),
+    ("C", "Whp1", "S"),
     ("Q", "Whp0"),
-    ("C", "hs0", "S"),
+    ("C", "hs0", "V"),
     ("Q", "Whp1"),
-    ("T", "Vhp0", 7),
+    ("T", "Vhp0", 7, 1),
     ("Q", "hs0"),
-    ("T", "Vhp1", 4),
-    ("C", "Vhp0", "S"),
-    ("T", "ha0", 5),
-    ("C", "Vhp1", "V"),
+    ("T", "Vhp1", 4, 1),
+    ("C", "Vhp0", "V"),
+    ("T", "ha0", 5, 1),
+    ("C", "Vhp1", "S"),
     ("MA", 0),
     ("Q", "Vhp0"),
     ("C", "ha0", "S"),
     ("Q", "Vhp1"),
     ("T", "x0k0", 6),
     ("Q", "ha0"),
-    ("T", "x0k1", 7),
-    ("C", "x0k0", "S"),
-    ("T", "Wx0k0", 4),
-    ("C", "x0k1", "V"),
-    ("T", "Wx0k1", 5),
-    ("Q", "x0k0"),
-    ("C", "Wx0k0", "S"),
-    ("Q", "x0k1"),
-    ("T", "Wx1k0", 6),
-    ("C", "Wx0k1", "V"),
-    ("T", "Wx1k1", 7),
-    ("Q", "Wx0k0"),
-    ("C", "Wx1k0", "S"),
-    ("Q", "Wx0k1"),
-    ("T", "Vhh0", 4),
-    ("C", "Wx1k1", "S"),
-    ("Q", "Wx1k0"),
-    ("T", "Vhh1", 5),
-    ("C", "Vhh0", "S"),
-    ("Q", "Wx1k1"),
+    ("T", "x0k1", 7, 1),
+    ("C", "x0k0", "V"),
     ("MA", 1),
-    ("C", "Vhh1", "V"),
+    ("C", "x0k1", "V"),
+    ("T", "Wx0k0", 4),
+    ("Q", "x0k0"),
+    ("Q", "x0k1"),
+    ("T", "Wx0k1", 5, 1),
+    ("C", "Wx0k0", "V"),
+    ("T", "Wx1k0", 6),
+    ("C", "Wx0k1", "S"),
+    ("T", "Wx1k1", 7, 1),
+    ("Q", "Wx0k0"),
+    ("C", "Wx1k0", "V"),
+    ("T", "Vhh0", 4),
+    ("T", "Vhh1", 5, 1),
+    ("Q", "Wx0k1"),
     ("T", "hs1", 6),
+    ("Q", "Wx1k0"),
+    ("C", "Vhh1", "S"),
+    ("C", "Wx1k1", "V"),
+    ("MA", 2),
+    ("C", "Vhh0", "V"),
+    ("T", "ha1", 7),
+    ("SA", 0),
+    ("Q", "Wx1k1"),
+    ("SA", 1),
+    ("T", "x1k0", 4),
     ("Q", "Vhh0"),
     ("Q", "Vhh1"),
-    ("MA", 2),
-    ("C", "hs1", "S"),
-    ("MA", 3),
-    ("SA", 0),
-    ("Q", "hs1"),
-    ("T", "ha1", 7),
-    ("SA", 1),
-    ("SA", 2),
-    ("T", "x1k0", 4),
-    ("SA", 3),
-    ("C", "ha1", "S"),
-    ("PR", 0, 1),
     ("T", "x1k1", 5),
+    ("C", "hs1", "V"),
     ("C", "x1k0", "S"),
-    ("PR", 1, 1),
-    ("T", "hs2", 6),
+    ("MA", 3),
+    ("C", "ha1", "V"),
     ("C", "x1k1", "S"),
-    ("QG", 0, 1),
+    ("T", "hs2", 6),
+    ("Q", "hs1"),
+    ("SA", 2),
     ("T", "ha2", 7),
-    ("QG", 1, 1),
     ("Q", "ha1"),
     ("C", "hs2", "S"),
     ("Q", "x1k0"),
     ("T", "x2k0", 4),
     ("Q", "x1k1"),
-    ("C", "ha2", "S"),
-    ("Q", "hs2"),
+    ("SA", 3),
     ("T", "x2k1", 5),
+    ("Q", "hs2"),
     ("C", "x2k0", "S"),
-    ("Q", "ha2"),
     ("T", "hs3", 6),
-    ("C", "x2k1", "S"),
-    ("Q", "x2k0"),
-    ("T", "ha3", 7),
-    ("C", "hs3", "S"),
-    ("Q", "x2k1"),
-    ("TX", 6, 4),
-    ("C", "ha3", "S"),
-    ("Q", "hs3"),
-    ("TX", 7, 5),
-    ("CX", 6, "S"),
-    ("Q", "ha3"),
-    ("S2", 0, 2),
-    ("S2", 1, 3),
-    ("CX", 7, "S"),
-    ("QX", 6),
+    ("C", "ha2", "V"),
     ("MB", 1, 0),
-    ("OC", 0, "S"),
-    ("OC", 1, "V"),
-    ("QX", 7),
-    ("ST", 0, 2),
+    ("C", "hs3", "S"),
+    ("Q", "x2k0"),
+    ("Q", "ha2"),
+    ("C", "x2k1", "V"),
     ("MB", 1, 1),
     ("SB", 1, 0),
-    ("MB", 2, 0),
+    ("Q", "hs3"),
+    ("Q", "x2k1"),
+    ("PR", 0, 1),
+    ("T", "ha3", 7),
     ("SB", 1, 1),
-    ("PR", 2, 1),
+    ("T", "x3k0", 4),
+    ("QG", 0, 1),
+    ("PR", 1, 1),
+    ("T", "x3k1", 5),
+    ("C", "ha3", "S"),
+    ("S2", 0, 2),
+    ("QG", 1, 1),
+    ("C", "x3k0", "S"),
+    ("MB", 2, 0),
+    ("Q", "ha3"),
+    ("C", "x3k1", "S"),
+    ("Q", "x3k0"),
+    ("OC", 0, "S"),
+    ("S2", 1, 3),
+    ("Q", "x3k1"),
     ("MB", 2, 1),
     ("SB", 2, 0),
-    ("PR", 3, 1),
-    ("QG", 2, 1),
-    ("MD", 6, 0),
-    ("QG", 3, 1),
+    ("OC", 1, "V"),
+    ("PR", 2, 1),
+    ("ST", 0, 2),
+    ("MB", 3, 0),
     ("SB", 2, 1),
-    ("PR", 4, 1),
+    ("QG", 2, 1),
+    ("PR", 3, 1),
     ("S2", 2, 2),
-    ("S2", 3, 3),
-    ("SD", 6),
-    ("PR", 5, 1),
-    ("MD", 7, 1),
+    ("QG", 3, 1),
+    ("PR", 4, 1),
+    ("MB", 3, 1),
+    ("SB", 3, 0),
     ("OC", 2, "S"),
-    ("OC", 3, "V"),
     ("QG", 4, 1),
-    ("ST", 2, 2),
-    ("QG", 5, 1),
-    ("PR", 6, 1),
+    ("PR", 5, 1),
+    ("S2", 3, 3),
     ("S2", 4, 2),
-    ("SD", 7),
+    ("SB", 3, 1),
+    ("QG", 5, 1),
+    ("OC", 3, "V"),
+    ("OC", 4, "S"),
+    ("PR", 6, 1),
+    ("ST", 2, 2),
     ("S2", 5, 3),
     ("QG", 6, 1),
-    ("OC", 4, "S"),
+    ("OC", 5, "S"),
     ("PR", 7, 1),
     ("S2", 6, 2),
-    ("OC", 5, "V"),
-    ("OC", 6, "S"),
-    ("QG", 7, 1),
     ("ST", 4, 2),
+    ("QG", 7, 1),
+    ("OC", 6, "S"),
     ("S2", 7, 3),
-    ("OC", 7, "V"),
+    ("OC", 7, "S"),
     ("ST", 6, 1),
     ("ST", 7, 1),
 ]
@@ -182,6 +182,7 @@ def tile_updatespeaker_pa_kernel(
         ident = keep.tile([P, P], F32, name="ident")
         warm_in = keep.tile([P, 1], F32, name="warm_in")
         warm_out = keep.tile([P, 1], F32, name="warm_out")
+        zeros = keep.tile([P, 512], BF16, name="zeros")
 
         whp_raw = keep.tile([P, 4, 512], BF16, name="whp_raw")
         vhp_raw = keep.tile([P, 4, 512], BF16, name="vhp_raw")
@@ -191,12 +192,12 @@ def tile_updatespeaker_pa_kernel(
         ha_raw = keep.tile([P, 8, 512], BF16, name="ha_raw")
         x_raw = keep.tile([P, 8, 1024], BF16, name="x_raw")
 
-        w_grp = keep.tile([P, 5, 512, 2], F32, name="w_grp", align_bytes=64)
-        w_codes = keep.tile([P, 5, 512], U32, name="w_codes", align_bytes=64)
-        w_scl = keep.tile([P, 5, 512], U8, name="w_scl", align_bytes=64)
-        a_grp = keep.tile([P, 4, 1024, 2], F32, name="a_grp", align_bytes=64)
-        a_codes = keep.tile([P, 4, 1024], U32, name="a_codes", align_bytes=64)
-        a_scl = keep.tile([P, 4, 1024], U8, name="a_scl", align_bytes=64)
+        w_grp = [keep.tile([P, 512, 2], F32, name="w_grp%d" % s, align_bytes=64) for s in range(5)]
+        w_codes = [keep.tile([P, 512], U32, name="w_codes%d" % s, align_bytes=64) for s in range(5)]
+        w_scl = [keep.tile([P, 512], U8, name="w_scl%d" % s, align_bytes=64) for s in range(5)]
+        a_grp = [keep.tile([P, 1024, 2], F32, name="a_grp%d" % s, align_bytes=64) for s in range(4)]
+        a_codes = [keep.tile([P, 1024], U32, name="a_codes%d" % s, align_bytes=64) for s in range(4)]
+        a_scl = [keep.tile([P, 1024], U8, name="a_scl%d" % s, align_bytes=64) for s in range(4)]
         sig = keep.tile([P, 4, 1024], F32, name="sig")
         g_grp = keep.tile([P, 1024, 4], BF16, name="g_grp", align_bytes=64)
         g_codes = keep.tile([P, 1024], U32, name="g_codes", align_bytes=64)
@@ -221,21 +222,19 @@ def tile_updatespeaker_pa_kernel(
             loads["hs%d" % j] = (hs_raw[:, 2 * j : 2 * j + 2, :], a_rows(spk_vectors)[:, 2 * j : 2 * j + 2, :])
             loads["ha%d" % j] = (ha_raw[:, 2 * j : 2 * j + 2, :], a_rows(adr_vectors)[:, 2 * j : 2 * j + 2, :])
             loads["x%d" % j] = (x_raw[:, 2 * j : 2 * j + 2, :], a_rows(encoder_hidden)[:, 2 * j : 2 * j + 2, :])
-        for r in range(8):
-            loads["x%ds" % r] = (x_raw[:, r : r + 1, :], a_rows(encoder_hidden)[:, r : r + 1, :])
 
         units = {}
         for h in range(2):
-            units["Whp%d" % h] = (whp_raw, 2 * h, 0, w_grp, w_codes, w_scl, 0, 256 * h)
-            units["Vhp%d" % h] = (vhp_raw, 2 * h, 0, w_grp, w_codes, w_scl, 1, 256 * h)
-            units["Vhh%d" % h] = (vhh_raw, 2 * h, 0, w_grp, w_codes, w_scl, 4, 256 * h)
+            units["Whp%d" % h] = (whp_raw, 2 * h, 0, w_grp[0], w_codes[0], w_scl[0], 256 * h)
+            units["Vhp%d" % h] = (vhp_raw, 2 * h, 0, w_grp[1], w_codes[1], w_scl[1], 256 * h)
+            units["Vhh%d" % h] = (vhh_raw, 2 * h, 0, w_grp[4], w_codes[4], w_scl[4], 256 * h)
             for g in range(2):
-                units["Wx%dk%d" % (h, g)] = (wxp_raw, 2 * h, 256 * g, w_grp, w_codes, w_scl, 2 + g, 256 * h)
+                units["Wx%dk%d" % (h, g)] = (wxp_raw, 2 * h, 256 * g, w_grp[2 + g], w_codes[2 + g], w_scl[2 + g], 256 * h)
         for j in range(4):
-            units["hs%d" % j] = (hs_raw, 2 * j, 0, a_grp, a_codes, a_scl, 0, 256 * j)
-            units["ha%d" % j] = (ha_raw, 2 * j, 0, a_grp, a_codes, a_scl, 1, 256 * j)
+            units["hs%d" % j] = (hs_raw, 2 * j, 0, a_grp[0], a_codes[0], a_scl[0], 256 * j)
+            units["ha%d" % j] = (ha_raw, 2 * j, 0, a_grp[1], a_codes[1], a_scl[1], 256 * j)
             for g in range(2):
-                units["x%dk%d" % (j, g)] = (x_raw, 2 * j, 256 * g, a_grp, a_codes, a_scl, 2 + g, 256 * j)
+                units["x%dk%d" % (j, g)] = (x_raw, 2 * j, 256 * g, a_grp[2 + g], a_codes[2 + g], a_scl[2 + g], 256 * j)
 
         live = {}
 
@@ -245,20 +244,15 @@ def tile_updatespeaker_pa_kernel(
         def mx(dst, s, t, c0, n, start, stop):
             nc.tensor.matmul_mx(
                 out=dst,
-                lhsT=w_codes[:, s, 128 * t : 128 * t + 128].bitcast(FP8X4),
-                lhsT_scale=w_scl[:, s, 128 * t : 128 * t + 128],
-                rhs=a_codes[:, s, c0 : c0 + n].bitcast(FP8X4),
-                rhs_scale=a_scl[:, s, c0 : c0 + n],
+                lhsT=w_codes[s][:, 128 * t : 128 * t + 128].bitcast(FP8X4),
+                lhsT_scale=w_scl[s][:, 128 * t : 128 * t + 128],
+                rhs=a_codes[s][:, c0 : c0 + n].bitcast(FP8X4),
+                rhs_scale=a_scl[s][:, c0 : c0 + n],
                 start=start,
                 stop=stop,
             )
 
-        def copy_out(eng, dst, src):
-            if eng == "V":
-                nc.vector.tensor_copy(out=dst, in_=src)
-            else:
-                nc.scalar.copy(out=dst, in_=src)
-
+        nc.vector.memset(zeros[:], 0.0)
         nc.vector.memset(warm_in[:], 0.0)
         make_identity(nc, ident[:])
         nc.scalar.activation(out=warm_out[:], in_=warm_in[:], func=SIGMOID)
@@ -267,10 +261,22 @@ def tile_updatespeaker_pa_kernel(
             kind = st[0]
             if kind == "L":
                 nc.sync.dma_start(out=loads[st[1]][0], in_=loads[st[1]][1])
+            elif kind == "W":
+                bk = bank(st[1], [P, 512], "dummy")
+                for i in range(st[2]):
+                    nc.tensor.matmul(out=bk[:], lhsT=zeros[:, 0:128], rhs=zeros[:], start=True, stop=True)
             elif kind == "T":
-                raw, row, w0, grp, codes, scl, s, c0 = units[st[1]]
+                raw, row, w0, grp, codes, scl, c0 = units[st[1]]
                 bk = bank(st[2], [P, 2, 256], "tp_" + st[1])
                 words = raw[:].bitcast(F32)
+                if len(st) > 3:
+                    nc.tensor.matmul(
+                        out=bk[:].rearrange("p u c -> p (u c)"),
+                        lhsT=raw[:, row, 0:128],
+                        rhs=raw[:, row, 0:512],
+                        start=True,
+                        stop=True,
+                    )
                 for half in range(2):
                     for i in range(2):
                         nc.tensor.transpose(
@@ -280,39 +286,19 @@ def tile_updatespeaker_pa_kernel(
                         )
                 live[st[1]] = bk
             elif kind == "C":
-                raw, row, w0, grp, codes, scl, s, c0 = units[st[1]]
-                copy_out(st[2], grp[:, s, c0 : c0 + 256, :], live[st[1]][:].rearrange("p u c -> p c u"))
+                raw, row, w0, grp, codes, scl, c0 = units[st[1]]
+                src = live[st[1]][:].rearrange("p u c -> p c u")
+                if st[2] == "V":
+                    nc.vector.tensor_copy(out=grp[:, c0 : c0 + 256, :], in_=src)
+                else:
+                    nc.scalar.copy(out=grp[:, c0 : c0 + 256, :], in_=src)
             elif kind == "Q":
-                raw, row, w0, grp, codes, scl, s, c0 = units[st[1]]
+                raw, row, w0, grp, codes, scl, c0 = units[st[1]]
                 nc.vector.quantize_mx(
-                    out=codes[:, s, c0 : c0 + 256].bitcast(FP8X4),
-                    scales=scl[:, s, c0 : c0 + 256],
-                    in_=grp[:].bitcast(BF16)[:, s, c0 : c0 + 256, :].rearrange("p c t -> p (c t)"),
+                    out=codes[:, c0 : c0 + 256].bitcast(FP8X4),
+                    scales=scl[:, c0 : c0 + 256],
+                    in_=grp[:].bitcast(BF16)[:, c0 : c0 + 256, :].rearrange("p c t -> p (c t)"),
                 )
-            elif kind == "TX":
-                r = st[1]
-                bk = bank(st[2], [P, 2, 2, 128], "tpx_%d" % r)
-                words = x_raw[:].bitcast(F32)
-                for g in range(2):
-                    for half in range(2):
-                        w0 = 256 * g + 128 * half
-                        nc.tensor.transpose(bk[:, g, half, :], words[:, r, w0 : w0 + 128], ident[:])
-                live["x%ds" % r] = bk
-            elif kind == "CX":
-                r = st[1]
-                copy_out(
-                    st[2],
-                    a_grp[:, 2:4, 128 * r : 128 * r + 128, :],
-                    live["x%ds" % r][:].rearrange("p g u c -> p g c u"),
-                )
-            elif kind == "QX":
-                r = st[1]
-                for s in (2, 3):
-                    nc.vector.quantize_mx(
-                        out=a_codes[:, s, 128 * r : 128 * r + 128].bitcast(FP8X4),
-                        scales=a_scl[:, s, 128 * r : 128 * r + 128],
-                        in_=a_grp[:].bitcast(BF16)[:, s, 128 * r : 128 * r + 128, :].rearrange("p c t -> p (c t)"),
-                    )
             elif kind == "MA":
                 s = st[1]
                 if s == 0:
@@ -342,24 +328,12 @@ def tile_updatespeaker_pa_kernel(
                     in_=live["gate%d_%d" % (j, h)][:],
                     func=SIGMOID,
                 )
-            elif kind == "MD":
-                r = st[1]
-                bk = bank(st[2], [P, 4, 128], "gater_%d" % r)
-                for t in range(4):
-                    for s in range(4):
-                        mx(bk[:, t, :], s, t, 128 * r, 128, s == 0, s == 3)
-                live["gater_%d" % r] = bk
-            elif kind == "SD":
-                r = st[1]
-                nc.scalar.activation(
-                    out=sig[:, :, 128 * r : 128 * r + 128], in_=live["gater_%d" % r][:], func=SIGMOID
-                )
             elif kind == "PR":
                 c0, n = 128 * st[1], 128 * st[2]
                 nc.vector.tensor_tensor(
                     out=g_grp[:, c0 : c0 + n, :],
                     in0=sig[:, :, c0 : c0 + n].rearrange("p t b -> p b t"),
-                    in1=a_grp[:].bitcast(BF16)[:, 1, c0 : c0 + n, :],
+                    in1=a_grp[1][:].bitcast(BF16)[:, c0 : c0 + n, :],
                     op=MULT,
                 )
             elif kind == "QG":
@@ -376,15 +350,18 @@ def tile_updatespeaker_pa_kernel(
                     out=bk[:],
                     lhsT=g_codes[:, 128 * r : 128 * r + 128].bitcast(FP8X4),
                     lhsT_scale=g_scl[:, 128 * r : 128 * r + 128],
-                    rhs=w_codes[:, 4, :].bitcast(FP8X4),
-                    rhs_scale=w_scl[:, 4, :],
+                    rhs=w_codes[4][:].bitcast(FP8X4),
+                    rhs_scale=w_scl[4][:],
                     start=True,
                     stop=True,
                 )
                 live["out_%d" % r] = bk
             elif kind == "OC":
                 r = st[1]
-                copy_out(st[2], o_sb[:, r, :], live["out_%d" % r][:])
+                if st[2] == "V":
+                    nc.vector.tensor_copy(out=o_sb[:, r, :], in_=live["out_%d" % r][:])
+                else:
+                    nc.scalar.copy(out=o_sb[:, r, :], in_=live["out_%d" % r][:])
             elif kind == "ST":
                 r0, n = st[1], st[2]
                 nc.sync.dma_start(

@@ -10,165 +10,13 @@ U8 = mybir.dt.uint8
 FP8X4 = mybir.dt.float8_e4m3fn_x4
 SIGMOID = mybir.ActivationFunctionType.Sigmoid
 MULT = mybir.AluOpType.mult
-P = 128
-FLOPS = 2 * 1024 * 512 * (1024 + 512 + 512 + 512)
 
-STEPS = [
-    ("L", "Whp0"),
-    ("L", "Whp1"),
-    ("L", "hs0"),
-    ("L", "Vhp"),
-    ("L", "ha0"),
-    ("L", "x0"),
-    ("L", "Wx0"),
-    ("L", "Wx1"),
-    ("L", "Vhh"),
-    ("L", "hs1"),
-    ("L", "ha1"),
-    ("L", "x1"),
-    ("L", "hs2"),
-    ("L", "ha2"),
-    ("L", "x2"),
-    ("L", "hs3"),
-    ("L", "ha3"),
-    ("L", "x3"),
-    ("W", 7, 4),
-    ("T", "Whp0", 4, 1),
-    ("T", "Whp1", 5, 1),
-    ("C", "Whp0", "S"),
-    ("T", "hs0", 6, 1),
-    ("C", "Whp1", "S"),
-    ("Q", "Whp0"),
-    ("C", "hs0", "V"),
-    ("Q", "Whp1"),
-    ("T", "Vhp0", 7, 1),
-    ("Q", "hs0"),
-    ("T", "Vhp1", 4, 1),
-    ("C", "Vhp0", "V"),
-    ("T", "ha0", 5, 1),
-    ("C", "Vhp1", "S"),
-    ("MA", 0),
-    ("Q", "Vhp0"),
-    ("C", "ha0", "S"),
-    ("Q", "Vhp1"),
-    ("T", "x0k0", 6),
-    ("Q", "ha0"),
-    ("T", "x0k1", 7, 1),
-    ("C", "x0k0", "V"),
-    ("MA", 1),
-    ("C", "x0k1", "V"),
-    ("T", "Wx0k0", 4),
-    ("Q", "x0k0"),
-    ("Q", "x0k1"),
-    ("T", "Wx0k1", 5, 1),
-    ("C", "Wx0k0", "V"),
-    ("T", "Wx1k0", 6),
-    ("C", "Wx0k1", "S"),
-    ("T", "Wx1k1", 7, 1),
-    ("Q", "Wx0k0"),
-    ("C", "Wx1k0", "V"),
-    ("T", "Vhh0", 4),
-    ("T", "Vhh1", 5, 1),
-    ("Q", "Wx0k1"),
-    ("T", "hs1", 6),
-    ("Q", "Wx1k0"),
-    ("C", "Vhh1", "S"),
-    ("C", "Wx1k1", "V"),
-    ("MA", 2),
-    ("C", "Vhh0", "V"),
-    ("T", "ha1", 7),
-    ("SA", 0),
-    ("Q", "Wx1k1"),
-    ("SA", 1),
-    ("T", "x1k0", 4),
-    ("Q", "Vhh0"),
-    ("Q", "Vhh1"),
-    ("T", "x1k1", 5),
-    ("C", "hs1", "V"),
-    ("C", "x1k0", "S"),
-    ("MA", 3),
-    ("C", "ha1", "V"),
-    ("C", "x1k1", "S"),
-    ("T", "hs2", 6),
-    ("Q", "hs1"),
-    ("SA", 2),
-    ("T", "ha2", 7),
-    ("Q", "ha1"),
-    ("C", "hs2", "S"),
-    ("Q", "x1k0"),
-    ("T", "x2k0", 4),
-    ("Q", "x1k1"),
-    ("SA", 3),
-    ("T", "x2k1", 5),
-    ("Q", "hs2"),
-    ("C", "x2k0", "S"),
-    ("T", "hs3", 6),
-    ("C", "ha2", "V"),
-    ("MB", 1, 0),
-    ("C", "hs3", "S"),
-    ("Q", "x2k0"),
-    ("Q", "ha2"),
-    ("C", "x2k1", "V"),
-    ("MB", 1, 1),
-    ("SB", 1, 0),
-    ("Q", "hs3"),
-    ("Q", "x2k1"),
-    ("PR", 0, 1),
-    ("T", "ha3", 7),
-    ("SB", 1, 1),
-    ("T", "x3k0", 4),
-    ("QG", 0, 1),
-    ("PR", 1, 1),
-    ("T", "x3k1", 5),
-    ("C", "ha3", "S"),
-    ("S2", 0, 2),
-    ("QG", 1, 1),
-    ("C", "x3k0", "S"),
-    ("MB", 2, 0),
-    ("Q", "ha3"),
-    ("C", "x3k1", "S"),
-    ("Q", "x3k0"),
-    ("OC", 0, "S"),
-    ("S2", 1, 3),
-    ("Q", "x3k1"),
-    ("MB", 2, 1),
-    ("SB", 2, 0),
-    ("OC", 1, "V"),
-    ("PR", 2, 1),
-    ("ST", 0, 2),
-    ("MB", 3, 0),
-    ("SB", 2, 1),
-    ("QG", 2, 1),
-    ("PR", 3, 1),
-    ("S2", 2, 2),
-    ("QG", 3, 1),
-    ("PR", 4, 1),
-    ("MB", 3, 1),
-    ("SB", 3, 0),
-    ("OC", 2, "S"),
-    ("QG", 4, 1),
-    ("PR", 5, 1),
-    ("S2", 3, 3),
-    ("S2", 4, 2),
-    ("SB", 3, 1),
-    ("QG", 5, 1),
-    ("OC", 3, "V"),
-    ("OC", 4, "S"),
-    ("PR", 6, 1),
-    ("ST", 2, 2),
-    ("S2", 5, 3),
-    ("QG", 6, 1),
-    ("OC", 5, "S"),
-    ("PR", 7, 1),
-    ("S2", 6, 2),
-    ("ST", 4, 2),
-    ("QG", 7, 1),
-    ("OC", 6, "S"),
-    ("S2", 7, 3),
-    ("OC", 7, "S"),
-    ("ST", 6, 1),
-    ("ST", 7, 1),
-]
+P = 128
+B, HID, UD = 1024, 1024, 512
+ROW_TILES = B // P
+CHUNK = 256
+CHUNKS = B // CHUNK
+FLOPS = 2 * B * UD * (HID + UD + UD + UD)
 
 
 def tile_updatespeaker_pa_kernel(
@@ -177,193 +25,159 @@ def tile_updatespeaker_pa_kernel(
     nc = tc.nc
     with ExitStack() as ctx:
         keep = ctx.enter_context(tc.tile_pool(name="keep", bufs=1))
-        psum = ctx.enter_context(tc.psum_pool(name="psum", bufs=1))
+        tp_psum = ctx.enter_context(tc.psum_pool(name="tp_psum", bufs=4))
+        gate_psum = ctx.enter_context(tc.psum_pool(name="gate_psum", bufs=2))
+        out_psum = ctx.enter_context(tc.psum_pool(name="out_psum", bufs=2))
 
         ident = keep.tile([P, P], F32, name="ident")
         warm_in = keep.tile([P, 1], F32, name="warm_in")
         warm_out = keep.tile([P, 1], F32, name="warm_out")
-        zeros = keep.tile([P, 512], BF16, name="zeros")
 
-        whp_raw = keep.tile([P, 4, 512], BF16, name="whp_raw")
-        vhp_raw = keep.tile([P, 4, 512], BF16, name="vhp_raw")
-        vhh_raw = keep.tile([P, 4, 512], BF16, name="vhh_raw")
-        wxp_raw = keep.tile([P, 4, 1024], BF16, name="wxp_raw")
-        hs_raw = keep.tile([P, 8, 512], BF16, name="hs_raw")
-        ha_raw = keep.tile([P, 8, 512], BF16, name="ha_raw")
-        x_raw = keep.tile([P, 8, 1024], BF16, name="x_raw")
+        whp_raw = keep.tile([P, 4, UD], BF16, name="whp_raw")
+        vhp_raw = keep.tile([P, 4, UD], BF16, name="vhp_raw")
+        wxp_raw = keep.tile([P, 4, HID], BF16, name="wxp_raw")
+        vhh_raw = keep.tile([P, 4, UD], BF16, name="vhh_raw")
+        hs_raw = keep.tile([P, ROW_TILES, UD], BF16, name="hs_raw")
+        ha_raw = keep.tile([P, ROW_TILES, UD], BF16, name="ha_raw")
+        x_raw = keep.tile([P, ROW_TILES, HID], BF16, name="x_raw")
 
-        w_grp = [keep.tile([P, 512, 2], F32, name="w_grp%d" % s, align_bytes=64) for s in range(5)]
-        w_codes = [keep.tile([P, 512], U32, name="w_codes%d" % s, align_bytes=64) for s in range(5)]
-        w_scl = [keep.tile([P, 512], U8, name="w_scl%d" % s, align_bytes=64) for s in range(5)]
-        a_grp = [keep.tile([P, 1024, 2], F32, name="a_grp%d" % s, align_bytes=64) for s in range(4)]
-        a_codes = [keep.tile([P, 1024], U32, name="a_codes%d" % s, align_bytes=64) for s in range(4)]
-        a_scl = [keep.tile([P, 1024], U8, name="a_scl%d" % s, align_bytes=64) for s in range(4)]
-        sig = keep.tile([P, 4, 1024], F32, name="sig")
-        g_grp = keep.tile([P, 1024, 4], BF16, name="g_grp", align_bytes=64)
-        g_codes = keep.tile([P, 1024], U32, name="g_codes", align_bytes=64)
-        g_scl = keep.tile([P, 1024], U8, name="g_scl", align_bytes=64)
-        o_sb = keep.tile([P, 8, 512], F32, name="o_sb")
+        w_pairs = keep.tile([P, 5, UD, 2], F32, name="w_pairs", align_bytes=64)
+        w_codes = keep.tile([P, 5, UD], U32, name="w_codes", align_bytes=64)
+        w_scales = keep.tile([P, 5, UD], U8, name="w_scales", align_bytes=64)
+        a_pairs = keep.tile([P, 4, B, 2], F32, name="a_pairs", align_bytes=64)
+        a_codes = keep.tile([P, 4, B], U32, name="a_codes", align_bytes=64)
+        a_scales = keep.tile([P, 4, B], U8, name="a_scales", align_bytes=64)
+        gate = keep.tile([P, 4, B], F32, name="gate")
+        g_vals = keep.tile([P, B, 4], BF16, name="g_vals", align_bytes=64)
+        g_codes = keep.tile([P, B], U32, name="g_codes", align_bytes=64)
+        g_scales = keep.tile([P, B], U8, name="g_scales", align_bytes=64)
+        o_rows = keep.tile([P, ROW_TILES, UD], F32, name="o_rows")
 
-        def w_rows(w):
+        def gate_weight_rows(w):
             return w.rearrange("(u p e) k -> p u e k", u=2, e=2)
 
-        def a_rows(a):
-            return a.rearrange("(p r) k -> p r k", r=8)
+        def batch_rows(a):
+            return a.rearrange("(p r) k -> p r k", r=ROW_TILES)
 
-        loads = {
-            "Whp0": (whp_raw[:, 0:2, :], w_rows(WA_hp)[:, 0, :, :]),
-            "Whp1": (whp_raw[:, 2:4, :], w_rows(WA_hp)[:, 1, :, :]),
-            "Vhp": (vhp_raw[:].rearrange("p (u e) k -> p u e k", u=2), w_rows(VA_hp)),
-            "Wx0": (wxp_raw[:, 0:2, :], w_rows(WA_xp)[:, 0, :, :]),
-            "Wx1": (wxp_raw[:, 2:4, :], w_rows(WA_xp)[:, 1, :, :]),
-            "Vhh": (vhh_raw[:], VA_hh.rearrange("(j p) k -> p j k", p=P)),
-        }
-        for j in range(4):
-            loads["hs%d" % j] = (hs_raw[:, 2 * j : 2 * j + 2, :], a_rows(spk_vectors)[:, 2 * j : 2 * j + 2, :])
-            loads["ha%d" % j] = (ha_raw[:, 2 * j : 2 * j + 2, :], a_rows(adr_vectors)[:, 2 * j : 2 * j + 2, :])
-            loads["x%d" % j] = (x_raw[:, 2 * j : 2 * j + 2, :], a_rows(encoder_hidden)[:, 2 * j : 2 * j + 2, :])
+        def load_gate_weight(raw, w):
+            for u in range(2):
+                nc.sync.dma_start(out=raw[:, 2 * u : 2 * u + 2, :], in_=gate_weight_rows(w)[:, u, :, :])
 
-        units = {}
-        for h in range(2):
-            units["Whp%d" % h] = (whp_raw, 2 * h, 0, w_grp[0], w_codes[0], w_scl[0], 256 * h)
-            units["Vhp%d" % h] = (vhp_raw, 2 * h, 0, w_grp[1], w_codes[1], w_scl[1], 256 * h)
-            units["Vhh%d" % h] = (vhh_raw, 2 * h, 0, w_grp[4], w_codes[4], w_scl[4], 256 * h)
-            for g in range(2):
-                units["Wx%dk%d" % (h, g)] = (wxp_raw, 2 * h, 256 * g, w_grp[2 + g], w_codes[2 + g], w_scl[2 + g], 256 * h)
-        for j in range(4):
-            units["hs%d" % j] = (hs_raw, 2 * j, 0, a_grp[0], a_codes[0], a_scl[0], 256 * j)
-            units["ha%d" % j] = (ha_raw, 2 * j, 0, a_grp[1], a_codes[1], a_scl[1], 256 * j)
-            for g in range(2):
-                units["x%dk%d" % (j, g)] = (x_raw, 2 * j, 256 * g, a_grp[2 + g], a_codes[2 + g], a_scl[2 + g], 256 * j)
+        def load_chunk(j):
+            rows = slice(2 * j, 2 * j + 2)
+            nc.sync.dma_start(out=hs_raw[:, rows, :], in_=batch_rows(spk_vectors)[:, rows, :])
+            nc.sync.dma_start(out=ha_raw[:, rows, :], in_=batch_rows(adr_vectors)[:, rows, :])
+            nc.sync.dma_start(out=x_raw[:, rows, :], in_=batch_rows(encoder_hidden)[:, rows, :])
 
-        live = {}
+        load_gate_weight(whp_raw, WA_hp)
+        load_gate_weight(vhp_raw, VA_hp)
+        load_gate_weight(wxp_raw, WA_xp)
+        load_chunk(0)
+        nc.sync.dma_start(out=vhh_raw[:], in_=VA_hh.rearrange("(j p) k -> p j k", p=P))
+        for j in range(1, CHUNKS):
+            load_chunk(j)
 
-        def bank(i, shape, label):
-            return psum.tile(shape, F32, tag="bank%d" % i, name=label)
+        nc.vector.memset(warm_in[:], 0.0)
+        nc.scalar.activation(out=warm_out[:], in_=warm_in[:], func=SIGMOID)
+        make_identity(nc, ident[:])
 
-        def mx(dst, s, t, c0, n, start, stop):
-            nc.tensor.matmul_mx(
-                out=dst,
-                lhsT=w_codes[s][:, 128 * t : 128 * t + 128].bitcast(FP8X4),
-                lhsT_scale=w_scl[s][:, 128 * t : 128 * t + 128],
-                rhs=a_codes[s][:, c0 : c0 + n].bitcast(FP8X4),
-                rhs_scale=a_scl[s][:, c0 : c0 + n],
-                start=start,
-                stop=stop,
+        copies = []
+
+        def leave_psum(dst, src):
+            if len(copies) % 3 == 1:
+                nc.vector.tensor_copy(out=dst, in_=src)
+            else:
+                nc.scalar.copy(out=dst, in_=src)
+            copies.append(1)
+
+        def to_mx(raw, row, k_pass, pairs, codes, scales, plane, col):
+            words = raw[:].bitcast(F32)
+            bank = tp_psum.tile([P, 2, CHUNK], F32, name="tp_bank")
+            for u in range(2):
+                first = 256 * k_pass + P * u
+                for i in range(2):
+                    nc.tensor.transpose(
+                        bank[:, u, P * i : P * i + P], words[:, row + i, first : first + P], ident[:]
+                    )
+            cols = slice(col, col + CHUNK)
+            leave_psum(pairs[:, plane, cols, :], bank[:].rearrange("p u c -> p c u"))
+            nc.vector.quantize_mx(
+                out=codes[:, plane, cols].bitcast(FP8X4),
+                scales=scales[:, plane, cols],
+                in_=pairs[:].bitcast(BF16)[:, plane, cols, :].rearrange("p c t -> p (c t)"),
             )
 
-        nc.vector.memset(zeros[:], 0.0)
-        nc.vector.memset(warm_in[:], 0.0)
-        make_identity(nc, ident[:])
-        nc.scalar.activation(out=warm_out[:], in_=warm_in[:], func=SIGMOID)
+        def weight_to_mx(raw, k_pass, plane):
+            for h in range(2):
+                to_mx(raw, 2 * h, k_pass, w_pairs, w_codes, w_scales, plane, CHUNK * h)
 
-        for st in STEPS:
-            kind = st[0]
-            if kind == "L":
-                nc.sync.dma_start(out=loads[st[1]][0], in_=loads[st[1]][1])
-            elif kind == "W":
-                bk = bank(st[1], [P, 512], "dummy")
-                for i in range(st[2]):
-                    nc.tensor.matmul(out=bk[:], lhsT=zeros[:, 0:128], rhs=zeros[:], start=True, stop=True)
-            elif kind == "T":
-                raw, row, w0, grp, codes, scl, c0 = units[st[1]]
-                bk = bank(st[2], [P, 2, 256], "tp_" + st[1])
-                words = raw[:].bitcast(F32)
-                if len(st) > 3:
-                    nc.tensor.matmul(
-                        out=bk[:].rearrange("p u c -> p (u c)"),
-                        lhsT=raw[:, row, 0:128],
-                        rhs=raw[:, row, 0:512],
-                        start=True,
-                        stop=True,
-                    )
-                for half in range(2):
-                    for i in range(2):
-                        nc.tensor.transpose(
-                            bk[:, half, 128 * i : 128 * i + 128],
-                            words[:, row + i, w0 + 128 * half : w0 + 128 * half + 128],
-                            ident[:],
-                        )
-                live[st[1]] = bk
-            elif kind == "C":
-                raw, row, w0, grp, codes, scl, c0 = units[st[1]]
-                src = live[st[1]][:].rearrange("p u c -> p c u")
-                if st[2] == "V":
-                    nc.vector.tensor_copy(out=grp[:, c0 : c0 + 256, :], in_=src)
-                else:
-                    nc.scalar.copy(out=grp[:, c0 : c0 + 256, :], in_=src)
-            elif kind == "Q":
-                raw, row, w0, grp, codes, scl, c0 = units[st[1]]
-                nc.vector.quantize_mx(
-                    out=codes[:, c0 : c0 + 256].bitcast(FP8X4),
-                    scales=scl[:, c0 : c0 + 256],
-                    in_=grp[:].bitcast(BF16)[:, c0 : c0 + 256, :].rearrange("p c t -> p (c t)"),
-                )
-            elif kind == "MA":
-                s = st[1]
-                if s == 0:
-                    for t in range(4):
-                        live["gate0_%d" % t] = bank(t, [P, 256], "gate0_%d" % t)
-                if s < 2:
-                    for t in range(4):
-                        mx(live["gate0_%d" % t][:], s, t, 0, 256, s == 0, False)
-                else:
-                    for t in (2 * s - 4, 2 * s - 3):
-                        mx(live["gate0_%d" % t][:], 2, t, 0, 256, False, False)
-                        mx(live["gate0_%d" % t][:], 3, t, 0, 256, False, True)
-            elif kind == "SA":
-                t = st[1]
-                nc.scalar.activation(out=sig[:, t, 0:256], in_=live["gate0_%d" % t][:], func=SIGMOID)
-            elif kind == "MB":
-                j, h = st[1], st[2]
-                bk = bank(h, [P, 2, 256], "gate%d_%d" % (j, h))
+        weight_to_mx(whp_raw, 0, 0)
+        weight_to_mx(vhp_raw, 0, 1)
+        weight_to_mx(wxp_raw, 0, 2)
+        weight_to_mx(wxp_raw, 1, 3)
+
+        def prepare(j):
+            to_mx(hs_raw, 2 * j, 0, a_pairs, a_codes, a_scales, 0, CHUNK * j)
+            to_mx(ha_raw, 2 * j, 0, a_pairs, a_codes, a_scales, 1, CHUNK * j)
+            to_mx(x_raw, 2 * j, 0, a_pairs, a_codes, a_scales, 2, CHUNK * j)
+            to_mx(x_raw, 2 * j, 1, a_pairs, a_codes, a_scales, 3, CHUNK * j)
+
+        def gated_state(j):
+            cols = slice(CHUNK * j, CHUNK * j + CHUNK)
+            for h in range(2):
+                sums = gate_psum.tile([P, 2, CHUNK], F32, name="sums")
                 for i in range(2):
+                    o_cols = slice(P * (2 * h + i), P * (2 * h + i) + P)
                     for s in range(4):
-                        mx(bk[:, i, :], s, 2 * h + i, 256 * j, 256, s == 0, s == 3)
-                live["gate%d_%d" % (j, h)] = bk
-            elif kind == "SB":
-                j, h = st[1], st[2]
-                nc.scalar.activation(
-                    out=sig[:, 2 * h : 2 * h + 2, 256 * j : 256 * j + 256],
-                    in_=live["gate%d_%d" % (j, h)][:],
-                    func=SIGMOID,
-                )
-            elif kind == "PR":
-                c0, n = 128 * st[1], 128 * st[2]
+                        nc.tensor.matmul_mx(
+                            out=sums[:, i, :],
+                            lhsT=w_codes[:, s, o_cols].bitcast(FP8X4),
+                            lhsT_scale=w_scales[:, s, o_cols],
+                            rhs=a_codes[:, s, cols].bitcast(FP8X4),
+                            rhs_scale=a_scales[:, s, cols],
+                            start=(s == 0),
+                            stop=(s == 3),
+                        )
+                nc.scalar.activation(out=gate[:, 2 * h : 2 * h + 2, cols], in_=sums[:], func=SIGMOID)
+            for r in (2 * j, 2 * j + 1):
+                b_cols = slice(P * r, P * r + P)
                 nc.vector.tensor_tensor(
-                    out=g_grp[:, c0 : c0 + n, :],
-                    in0=sig[:, :, c0 : c0 + n].rearrange("p t b -> p b t"),
-                    in1=a_grp[1][:].bitcast(BF16)[:, c0 : c0 + n, :],
+                    out=g_vals[:, b_cols, :],
+                    in0=gate[:, :, b_cols].rearrange("p t b -> p b t"),
+                    in1=a_pairs[:].bitcast(BF16)[:, 1, b_cols, :],
                     op=MULT,
                 )
-            elif kind == "QG":
-                c0, n = 128 * st[1], 128 * st[2]
                 nc.vector.quantize_mx(
-                    out=g_codes[:, c0 : c0 + n].bitcast(FP8X4),
-                    scales=g_scl[:, c0 : c0 + n],
-                    in_=g_grp[:, c0 : c0 + n, :].rearrange("p c t -> p (c t)"),
+                    out=g_codes[:, b_cols].bitcast(FP8X4),
+                    scales=g_scales[:, b_cols],
+                    in_=g_vals[:, b_cols, :].rearrange("p c t -> p (c t)"),
                 )
-            elif kind == "S2":
-                r = st[1]
-                bk = bank(st[2], [P, 512], "out_%d" % r)
+
+        def project(j):
+            for r in (2 * j, 2 * j + 1):
+                b_cols = slice(P * r, P * r + P)
+                proj = out_psum.tile([P, UD], F32, name="proj")
                 nc.tensor.matmul_mx(
-                    out=bk[:],
-                    lhsT=g_codes[:, 128 * r : 128 * r + 128].bitcast(FP8X4),
-                    lhsT_scale=g_scl[:, 128 * r : 128 * r + 128],
-                    rhs=w_codes[4][:].bitcast(FP8X4),
-                    rhs_scale=w_scl[4][:],
+                    out=proj[:],
+                    lhsT=g_codes[:, b_cols].bitcast(FP8X4),
+                    lhsT_scale=g_scales[:, b_cols],
+                    rhs=w_codes[:, 4, :].bitcast(FP8X4),
+                    rhs_scale=w_scales[:, 4, :],
                     start=True,
                     stop=True,
                 )
-                live["out_%d" % r] = bk
-            elif kind == "OC":
-                r = st[1]
-                if st[2] == "V":
-                    nc.vector.tensor_copy(out=o_sb[:, r, :], in_=live["out_%d" % r][:])
+                if r % 2 == 1:
+                    nc.vector.tensor_copy(out=o_rows[:, r, :], in_=proj[:])
                 else:
-                    nc.scalar.copy(out=o_sb[:, r, :], in_=live["out_%d" % r][:])
-            elif kind == "ST":
-                r0, n = st[1], st[2]
-                nc.sync.dma_start(
-                    out=out.rearrange("(p r) o -> p r o", r=8)[:, r0 : r0 + n, :], in_=o_sb[:, r0 : r0 + n, :]
-                )
+                    nc.scalar.copy(out=o_rows[:, r, :], in_=proj[:])
+                nc.sync.dma_start(out=batch_rows(out)[:, r : r + 1, :], in_=o_rows[:, r : r + 1, :])
+
+        prepare(0)
+        weight_to_mx(vhh_raw, 0, 4)
+        for j in range(CHUNKS + 2):
+            if j + 1 < CHUNKS:
+                prepare(j + 1)
+            if j < CHUNKS:
+                gated_state(j)
+            if j >= 2:
+                project(j - 2)

@@ -16,6 +16,7 @@ B, HID, UD = 1024, 1024, 512
 ROW_TILES = B // P
 CHUNK = 256
 CHUNKS = B // CHUNK
+LAG = 2
 FLOPS = 2 * B * UD * (HID + UD + UD + UD)
 
 
@@ -44,24 +45,22 @@ def tile_updatespeaker_pa_kernel(
         w_pairs = keep.tile([P, 5, UD, 2], F32, name="w_pairs", align_bytes=64)
         w_codes = keep.tile([P, 5, UD], U32, name="w_codes", align_bytes=64)
         w_scales = keep.tile([P, 5, UD], U8, name="w_scales", align_bytes=64)
-        a_pairs = keep.tile([P, 4, B, 2], F32, name="a_pairs", align_bytes=64)
-        a_codes = keep.tile([P, 4, B], U32, name="a_codes", align_bytes=64)
-        a_scales = keep.tile([P, 4, B], U8, name="a_scales", align_bytes=64)
-        gate = keep.tile([P, 4, B], F32, name="gate")
-        g_vals = keep.tile([P, B, 4], BF16, name="g_vals", align_bytes=64)
-        g_codes = keep.tile([P, B], U32, name="g_codes", align_bytes=64)
-        g_scales = keep.tile([P, B], U8, name="g_scales", align_bytes=64)
+        a_pairs = keep.tile([P, CHUNKS, 4, CHUNK, 2], F32, name="a_pairs", align_bytes=64)
+        a_codes = keep.tile([P, CHUNKS, 4, CHUNK], U32, name="a_codes", align_bytes=64)
+        a_scales = keep.tile([P, CHUNKS, 4, CHUNK], U8, name="a_scales", align_bytes=64)
+        gate = keep.tile([P, CHUNKS, 4, CHUNK], F32, name="gate")
+        g_vals = keep.tile([P, CHUNKS, CHUNK, 4], BF16, name="g_vals", align_bytes=64)
+        g_codes = keep.tile([P, CHUNKS, CHUNK], U32, name="g_codes", align_bytes=64)
+        g_scales = keep.tile([P, CHUNKS, CHUNK], U8, name="g_scales", align_bytes=64)
         o_rows = keep.tile([P, ROW_TILES, UD], F32, name="o_rows")
-
-        def gate_weight_rows(w):
-            return w.rearrange("(u p e) k -> p u e k", u=2, e=2)
 
         def batch_rows(a):
             return a.rearrange("(p r) k -> p r k", r=ROW_TILES)
 
         def load_gate_weight(raw, w):
+            rows = w.rearrange("(u p e) k -> p u e k", u=2, e=2)
             for u in range(2):
-                nc.sync.dma_start(out=raw[:, 2 * u : 2 * u + 2, :], in_=gate_weight_rows(w)[:, u, :, :])
+                nc.sync.dma_start(out=raw[:, 2 * u : 2 * u + 2, :], in_=rows[:, u, :, :])
 
         def load_chunk(j):
             rows = slice(2 * j, 2 * j + 2)
@@ -81,16 +80,9 @@ def tile_updatespeaker_pa_kernel(
         nc.scalar.activation(out=warm_out[:], in_=warm_in[:], func=SIGMOID)
         make_identity(nc, ident[:])
 
-        copies = []
+        banks_emptied = []
 
-        def leave_psum(dst, src):
-            if len(copies) % 3 == 1:
-                nc.vector.tensor_copy(out=dst, in_=src)
-            else:
-                nc.scalar.copy(out=dst, in_=src)
-            copies.append(1)
-
-        def to_mx(raw, row, k_pass, pairs, codes, scales, plane, col):
+        def turn(raw, row, k_pass, pairs):
             words = raw[:].bitcast(F32)
             bank = tp_psum.tile([P, 2, CHUNK], F32, name="tp_bank")
             for u in range(2):
@@ -99,31 +91,33 @@ def tile_updatespeaker_pa_kernel(
                     nc.tensor.transpose(
                         bank[:, u, P * i : P * i + P], words[:, row + i, first : first + P], ident[:]
                     )
-            cols = slice(col, col + CHUNK)
-            leave_psum(pairs[:, plane, cols, :], bank[:].rearrange("p u c -> p c u"))
-            nc.vector.quantize_mx(
-                out=codes[:, plane, cols].bitcast(FP8X4),
-                scales=scales[:, plane, cols],
-                in_=pairs[:].bitcast(BF16)[:, plane, cols, :].rearrange("p c t -> p (c t)"),
-            )
+            if len(banks_emptied) % 3 == 1:
+                nc.vector.tensor_copy(out=pairs, in_=bank[:].rearrange("p u c -> p c u"))
+            else:
+                nc.scalar.copy(out=pairs, in_=bank[:].rearrange("p u c -> p c u"))
+            banks_emptied.append(row)
 
         def weight_to_mx(raw, k_pass, plane):
             for h in range(2):
-                to_mx(raw, 2 * h, k_pass, w_pairs, w_codes, w_scales, plane, CHUNK * h)
-
-        weight_to_mx(whp_raw, 0, 0)
-        weight_to_mx(vhp_raw, 0, 1)
-        weight_to_mx(wxp_raw, 0, 2)
-        weight_to_mx(wxp_raw, 1, 3)
+                turn(raw, 2 * h, k_pass, w_pairs[:, plane, CHUNK * h : CHUNK * h + CHUNK, :])
+            nc.vector.quantize_mx(
+                out=w_codes[:, plane, :].bitcast(FP8X4),
+                scales=w_scales[:, plane, :],
+                in_=w_pairs[:].bitcast(BF16)[:, plane, :, :].rearrange("p c t -> p (c t)"),
+            )
 
         def prepare(j):
-            to_mx(hs_raw, 2 * j, 0, a_pairs, a_codes, a_scales, 0, CHUNK * j)
-            to_mx(ha_raw, 2 * j, 0, a_pairs, a_codes, a_scales, 1, CHUNK * j)
-            to_mx(x_raw, 2 * j, 0, a_pairs, a_codes, a_scales, 2, CHUNK * j)
-            to_mx(x_raw, 2 * j, 1, a_pairs, a_codes, a_scales, 3, CHUNK * j)
+            turn(hs_raw, 2 * j, 0, a_pairs[:, j, 0, :, :])
+            turn(ha_raw, 2 * j, 0, a_pairs[:, j, 1, :, :])
+            turn(x_raw, 2 * j, 0, a_pairs[:, j, 2, :, :])
+            turn(x_raw, 2 * j, 1, a_pairs[:, j, 3, :, :])
+            nc.vector.quantize_mx(
+                out=a_codes[:, j, :, :].rearrange("p s c -> p (s c)").bitcast(FP8X4),
+                scales=a_scales[:, j, :, :].rearrange("p s c -> p (s c)"),
+                in_=a_pairs[:].bitcast(BF16)[:, j, :, :, :].rearrange("p s c t -> p (s c t)"),
+            )
 
         def gated_state(j):
-            cols = slice(CHUNK * j, CHUNK * j + CHUNK)
             for h in range(2):
                 sums = gate_psum.tile([P, 2, CHUNK], F32, name="sums")
                 for i in range(2):
@@ -133,51 +127,53 @@ def tile_updatespeaker_pa_kernel(
                             out=sums[:, i, :],
                             lhsT=w_codes[:, s, o_cols].bitcast(FP8X4),
                             lhsT_scale=w_scales[:, s, o_cols],
-                            rhs=a_codes[:, s, cols].bitcast(FP8X4),
-                            rhs_scale=a_scales[:, s, cols],
+                            rhs=a_codes[:, j, s, :].bitcast(FP8X4),
+                            rhs_scale=a_scales[:, j, s, :],
                             start=(s == 0),
                             stop=(s == 3),
                         )
-                nc.scalar.activation(out=gate[:, 2 * h : 2 * h + 2, cols], in_=sums[:], func=SIGMOID)
-            for r in (2 * j, 2 * j + 1):
-                b_cols = slice(P * r, P * r + P)
-                nc.vector.tensor_tensor(
-                    out=g_vals[:, b_cols, :],
-                    in0=gate[:, :, b_cols].rearrange("p t b -> p b t"),
-                    in1=a_pairs[:].bitcast(BF16)[:, 1, b_cols, :],
-                    op=MULT,
-                )
-                nc.vector.quantize_mx(
-                    out=g_codes[:, b_cols].bitcast(FP8X4),
-                    scales=g_scales[:, b_cols],
-                    in_=g_vals[:, b_cols, :].rearrange("p c t -> p (c t)"),
-                )
+                nc.scalar.activation(out=gate[:, j, 2 * h : 2 * h + 2, :], in_=sums[:], func=SIGMOID)
+            nc.vector.tensor_tensor(
+                out=g_vals[:, j, :, :],
+                in0=gate[:, j, :, :].rearrange("p t b -> p b t"),
+                in1=a_pairs[:].bitcast(BF16)[:, j, 1, :, :],
+                op=MULT,
+            )
+            nc.vector.quantize_mx(
+                out=g_codes[:, j, :].bitcast(FP8X4),
+                scales=g_scales[:, j, :],
+                in_=g_vals[:, j, :, :].rearrange("p c t -> p (c t)"),
+            )
 
         def project(j):
-            for r in (2 * j, 2 * j + 1):
-                b_cols = slice(P * r, P * r + P)
+            for i in range(2):
+                r = 2 * j + i
                 proj = out_psum.tile([P, UD], F32, name="proj")
                 nc.tensor.matmul_mx(
                     out=proj[:],
-                    lhsT=g_codes[:, b_cols].bitcast(FP8X4),
-                    lhsT_scale=g_scales[:, b_cols],
+                    lhsT=g_codes[:, j, P * i : P * i + P].bitcast(FP8X4),
+                    lhsT_scale=g_scales[:, j, P * i : P * i + P],
                     rhs=w_codes[:, 4, :].bitcast(FP8X4),
                     rhs_scale=w_scales[:, 4, :],
                     start=True,
                     stop=True,
                 )
-                if r % 2 == 1:
+                if i == 1:
                     nc.vector.tensor_copy(out=o_rows[:, r, :], in_=proj[:])
                 else:
                     nc.scalar.copy(out=o_rows[:, r, :], in_=proj[:])
                 nc.sync.dma_start(out=batch_rows(out)[:, r : r + 1, :], in_=o_rows[:, r : r + 1, :])
 
+        weight_to_mx(whp_raw, 0, 0)
+        weight_to_mx(vhp_raw, 0, 1)
+        weight_to_mx(wxp_raw, 0, 2)
+        weight_to_mx(wxp_raw, 1, 3)
         prepare(0)
         weight_to_mx(vhh_raw, 0, 4)
-        for j in range(CHUNKS + 2):
+        for j in range(CHUNKS + LAG):
             if j + 1 < CHUNKS:
                 prepare(j + 1)
             if j < CHUNKS:
                 gated_state(j)
-            if j >= 2:
-                project(j - 2)
+            if j >= LAG:
+                project(j - LAG)

@@ -16,7 +16,6 @@ B, HID, UD = 1024, 1024, 512
 ROW_TILES = B // P
 CHUNK = 256
 CHUNKS = B // CHUNK
-LAG = 2
 FLOPS = 2 * B * UD * (HID + UD + UD + UD)
 
 
@@ -29,6 +28,7 @@ def tile_updatespeaker_pa_kernel(
         tp_psum = ctx.enter_context(tc.psum_pool(name="tp_psum", bufs=4))
         gate_psum = ctx.enter_context(tc.psum_pool(name="gate_psum", bufs=2))
         out_psum = ctx.enter_context(tc.psum_pool(name="out_psum", bufs=2))
+        ctx.enter_context(tc.manual_schedule())
 
         ident = keep.tile([P, P], F32, name="ident")
         warm_in = keep.tile([P, 1], F32, name="warm_in")
@@ -45,22 +45,24 @@ def tile_updatespeaker_pa_kernel(
         w_pairs = keep.tile([P, 5, UD, 2], F32, name="w_pairs", align_bytes=64)
         w_codes = keep.tile([P, 5, UD], U32, name="w_codes", align_bytes=64)
         w_scales = keep.tile([P, 5, UD], U8, name="w_scales", align_bytes=64)
-        a_pairs = keep.tile([P, CHUNKS, 4, CHUNK, 2], F32, name="a_pairs", align_bytes=64)
-        a_codes = keep.tile([P, CHUNKS, 4, CHUNK], U32, name="a_codes", align_bytes=64)
-        a_scales = keep.tile([P, CHUNKS, 4, CHUNK], U8, name="a_scales", align_bytes=64)
-        gate = keep.tile([P, CHUNKS, 4, CHUNK], F32, name="gate")
-        g_vals = keep.tile([P, CHUNKS, CHUNK, 4], BF16, name="g_vals", align_bytes=64)
-        g_codes = keep.tile([P, CHUNKS, CHUNK], U32, name="g_codes", align_bytes=64)
-        g_scales = keep.tile([P, CHUNKS, CHUNK], U8, name="g_scales", align_bytes=64)
+        a_pairs = keep.tile([P, 4, B, 2], F32, name="a_pairs", align_bytes=64)
+        a_codes = keep.tile([P, 4, B], U32, name="a_codes", align_bytes=64)
+        a_scales = keep.tile([P, 4, B], U8, name="a_scales", align_bytes=64)
+        gate = keep.tile([P, 4, B], F32, name="gate")
+        g_vals = keep.tile([P, B, 4], BF16, name="g_vals", align_bytes=64)
+        g_codes = keep.tile([P, B], U32, name="g_codes", align_bytes=64)
+        g_scales = keep.tile([P, B], U8, name="g_scales", align_bytes=64)
         o_rows = keep.tile([P, ROW_TILES, UD], F32, name="o_rows")
+
+        def gate_weight_rows(w):
+            return w.rearrange("(u p e) k -> p u e k", u=2, e=2)
 
         def batch_rows(a):
             return a.rearrange("(p r) k -> p r k", r=ROW_TILES)
 
         def load_gate_weight(raw, w):
-            rows = w.rearrange("(u p e) k -> p u e k", u=2, e=2)
             for u in range(2):
-                nc.sync.dma_start(out=raw[:, 2 * u : 2 * u + 2, :], in_=rows[:, u, :, :])
+                nc.sync.dma_start(out=raw[:, 2 * u : 2 * u + 2, :], in_=gate_weight_rows(w)[:, u, :, :])
 
         def load_chunk(j):
             rows = slice(2 * j, 2 * j + 2)
@@ -80,9 +82,26 @@ def tile_updatespeaker_pa_kernel(
         nc.scalar.activation(out=warm_out[:], in_=warm_in[:], func=SIGMOID)
         make_identity(nc, ident[:])
 
-        banks_emptied = []
+        copies = []
+        waiting = []
 
-        def turn(raw, row, k_pass, pairs):
+        def leave_psum(dst, src):
+            if len(copies) % 3 == 2:
+                nc.vector.tensor_copy(out=dst, in_=src)
+            else:
+                nc.scalar.copy(out=dst, in_=src)
+            copies.append(1)
+
+        def quantise_waiting(keep_back):
+            while len(waiting) > keep_back:
+                pairs, codes, scales, plane, cols = waiting.pop(0)
+                nc.vector.quantize_mx(
+                    out=codes[:, plane, cols].bitcast(FP8X4),
+                    scales=scales[:, plane, cols],
+                    in_=pairs[:].bitcast(BF16)[:, plane, cols, :].rearrange("p c t -> p (c t)"),
+                )
+
+        def to_mx(raw, row, k_pass, pairs, codes, scales, plane, col):
             words = raw[:].bitcast(F32)
             bank = tp_psum.tile([P, 2, CHUNK], F32, name="tp_bank")
             for u in range(2):
@@ -91,33 +110,30 @@ def tile_updatespeaker_pa_kernel(
                     nc.tensor.transpose(
                         bank[:, u, P * i : P * i + P], words[:, row + i, first : first + P], ident[:]
                     )
-            if len(banks_emptied) % 3 == 1:
-                nc.vector.tensor_copy(out=pairs, in_=bank[:].rearrange("p u c -> p c u"))
-            else:
-                nc.scalar.copy(out=pairs, in_=bank[:].rearrange("p u c -> p c u"))
-            banks_emptied.append(row)
+            cols = slice(col, col + CHUNK)
+            leave_psum(pairs[:, plane, cols, :], bank[:].rearrange("p u c -> p c u"))
+            waiting.append((pairs, codes, scales, plane, cols))
+            quantise_waiting(1)
 
         def weight_to_mx(raw, k_pass, plane):
             for h in range(2):
-                turn(raw, 2 * h, k_pass, w_pairs[:, plane, CHUNK * h : CHUNK * h + CHUNK, :])
-            nc.vector.quantize_mx(
-                out=w_codes[:, plane, :].bitcast(FP8X4),
-                scales=w_scales[:, plane, :],
-                in_=w_pairs[:].bitcast(BF16)[:, plane, :, :].rearrange("p c t -> p (c t)"),
-            )
+                to_mx(raw, 2 * h, k_pass, w_pairs, w_codes, w_scales, plane, CHUNK * h)
+
+        weight_to_mx(whp_raw, 0, 0)
+        weight_to_mx(vhp_raw, 0, 1)
+        weight_to_mx(wxp_raw, 0, 2)
+        weight_to_mx(wxp_raw, 1, 3)
 
         def prepare(j):
-            turn(hs_raw, 2 * j, 0, a_pairs[:, j, 0, :, :])
-            turn(ha_raw, 2 * j, 0, a_pairs[:, j, 1, :, :])
-            turn(x_raw, 2 * j, 0, a_pairs[:, j, 2, :, :])
-            turn(x_raw, 2 * j, 1, a_pairs[:, j, 3, :, :])
-            nc.vector.quantize_mx(
-                out=a_codes[:, j, :, :].rearrange("p s c -> p (s c)").bitcast(FP8X4),
-                scales=a_scales[:, j, :, :].rearrange("p s c -> p (s c)"),
-                in_=a_pairs[:].bitcast(BF16)[:, j, :, :, :].rearrange("p s c t -> p (s c t)"),
-            )
+            to_mx(hs_raw, 2 * j, 0, a_pairs, a_codes, a_scales, 0, CHUNK * j)
+            to_mx(ha_raw, 2 * j, 0, a_pairs, a_codes, a_scales, 1, CHUNK * j)
+            to_mx(x_raw, 2 * j, 0, a_pairs, a_codes, a_scales, 2, CHUNK * j)
+            to_mx(x_raw, 2 * j, 1, a_pairs, a_codes, a_scales, 3, CHUNK * j)
+            if j > 0:
+                quantise_waiting(0)
 
         def gated_state(j):
+            cols = slice(CHUNK * j, CHUNK * j + CHUNK)
             for h in range(2):
                 sums = gate_psum.tile([P, 2, CHUNK], F32, name="sums")
                 for i in range(2):
@@ -127,53 +143,52 @@ def tile_updatespeaker_pa_kernel(
                             out=sums[:, i, :],
                             lhsT=w_codes[:, s, o_cols].bitcast(FP8X4),
                             lhsT_scale=w_scales[:, s, o_cols],
-                            rhs=a_codes[:, j, s, :].bitcast(FP8X4),
-                            rhs_scale=a_scales[:, j, s, :],
+                            rhs=a_codes[:, s, cols].bitcast(FP8X4),
+                            rhs_scale=a_scales[:, s, cols],
                             start=(s == 0),
                             stop=(s == 3),
                         )
-                nc.scalar.activation(out=gate[:, j, 2 * h : 2 * h + 2, :], in_=sums[:], func=SIGMOID)
-            nc.vector.tensor_tensor(
-                out=g_vals[:, j, :, :],
-                in0=gate[:, j, :, :].rearrange("p t b -> p b t"),
-                in1=a_pairs[:].bitcast(BF16)[:, j, 1, :, :],
-                op=MULT,
-            )
-            nc.vector.quantize_mx(
-                out=g_codes[:, j, :].bitcast(FP8X4),
-                scales=g_scales[:, j, :],
-                in_=g_vals[:, j, :, :].rearrange("p c t -> p (c t)"),
-            )
+                nc.scalar.activation(out=gate[:, 2 * h : 2 * h + 2, cols], in_=sums[:], func=SIGMOID)
+            for r in (2 * j, 2 * j + 1):
+                b_cols = slice(P * r, P * r + P)
+                nc.vector.tensor_tensor(
+                    out=g_vals[:, b_cols, :],
+                    in0=gate[:, :, b_cols].rearrange("p t b -> p b t"),
+                    in1=a_pairs[:].bitcast(BF16)[:, 1, b_cols, :],
+                    op=MULT,
+                )
+                nc.vector.quantize_mx(
+                    out=g_codes[:, b_cols].bitcast(FP8X4),
+                    scales=g_scales[:, b_cols],
+                    in_=g_vals[:, b_cols, :].rearrange("p c t -> p (c t)"),
+                )
 
         def project(j):
-            for i in range(2):
-                r = 2 * j + i
+            for r in (2 * j, 2 * j + 1):
+                b_cols = slice(P * r, P * r + P)
                 proj = out_psum.tile([P, UD], F32, name="proj")
                 nc.tensor.matmul_mx(
                     out=proj[:],
-                    lhsT=g_codes[:, j, P * i : P * i + P].bitcast(FP8X4),
-                    lhsT_scale=g_scales[:, j, P * i : P * i + P],
+                    lhsT=g_codes[:, b_cols].bitcast(FP8X4),
+                    lhsT_scale=g_scales[:, b_cols],
                     rhs=w_codes[:, 4, :].bitcast(FP8X4),
                     rhs_scale=w_scales[:, 4, :],
                     start=True,
                     stop=True,
                 )
-                if i == 1:
+                if r % 2 == 1:
                     nc.vector.tensor_copy(out=o_rows[:, r, :], in_=proj[:])
                 else:
                     nc.scalar.copy(out=o_rows[:, r, :], in_=proj[:])
                 nc.sync.dma_start(out=batch_rows(out)[:, r : r + 1, :], in_=o_rows[:, r : r + 1, :])
 
-        weight_to_mx(whp_raw, 0, 0)
-        weight_to_mx(vhp_raw, 0, 1)
-        weight_to_mx(wxp_raw, 0, 2)
-        weight_to_mx(wxp_raw, 1, 3)
         prepare(0)
         weight_to_mx(vhh_raw, 0, 4)
-        for j in range(CHUNKS + LAG):
+        quantise_waiting(0)
+        for j in range(CHUNKS + 1):
             if j + 1 < CHUNKS:
                 prepare(j + 1)
             if j < CHUNKS:
                 gated_state(j)
-            if j >= LAG:
-                project(j - LAG)
+            if j >= 1:
+                project(j - 1)

from contextlib import ExitStack

import concourse.mybir as mybir
from concourse.masks import make_identity

F32 = mybir.dt.float32
BF16 = mybir.dt.bfloat16
U32 = mybir.dt.uint32
U8 = mybir.dt.uint8
FP8X4 = mybir.dt.float8_e4m3fn_x4
SIGMOID = mybir.ActivationFunctionType.Sigmoid
MULT = mybir.AluOpType.mult

P = 128
B, HID, UD = 1024, 1024, 512
ROW_TILES = B // P
CHUNK = 256
CHUNKS = B // CHUNK
FLOPS = 2 * B * UD * (HID + UD + UD + UD)


def tile_updatespeaker_pa_kernel(
    tc, encoder_hidden, spk_vectors, adr_vectors, WA_xp, WA_hp, VA_hp, VA_hh, out
):
    nc = tc.nc
    with ExitStack() as ctx:
        keep = ctx.enter_context(tc.tile_pool(name="keep", bufs=1))
        tp_psum = ctx.enter_context(tc.psum_pool(name="tp_psum", bufs=4))
        gate_psum = ctx.enter_context(tc.psum_pool(name="gate_psum", bufs=2))
        out_psum = ctx.enter_context(tc.psum_pool(name="out_psum", bufs=2))
        ctx.enter_context(tc.manual_schedule())

        ident = keep.tile([P, P], F32, name="ident")
        warm_in = keep.tile([P, 1], F32, name="warm_in")
        warm_out = keep.tile([P, 1], F32, name="warm_out")

        whp_raw = keep.tile([P, 4, UD], BF16, name="whp_raw")
        vhp_raw = keep.tile([P, 4, UD], BF16, name="vhp_raw")
        wxp_raw = keep.tile([P, 4, HID], BF16, name="wxp_raw")
        vhh_raw = keep.tile([P, 4, UD], BF16, name="vhh_raw")
        hs_raw = keep.tile([P, ROW_TILES, UD], BF16, name="hs_raw")
        ha_raw = keep.tile([P, ROW_TILES, UD], BF16, name="ha_raw")
        x_raw = keep.tile([P, ROW_TILES, HID], BF16, name="x_raw")

        w_pairs = keep.tile([P, 5, UD, 2], F32, name="w_pairs", align_bytes=64)
        w_codes = keep.tile([P, 5, UD], U32, name="w_codes", align_bytes=64)
        w_scales = keep.tile([P, 5, UD], U8, name="w_scales", align_bytes=64)
        a_pairs = keep.tile([P, 4, B, 2], F32, name="a_pairs", align_bytes=64)
        a_codes = keep.tile([P, 4, B], U32, name="a_codes", align_bytes=64)
        a_scales = keep.tile([P, 4, B], U8, name="a_scales", align_bytes=64)
        gate = keep.tile([P, 4, B], F32, name="gate")
        g_vals = keep.tile([P, B, 4], BF16, name="g_vals", align_bytes=64)
        g_codes = keep.tile([P, B], U32, name="g_codes", align_bytes=64)
        g_scales = keep.tile([P, B], U8, name="g_scales", align_bytes=64)
        o_rows = keep.tile([P, ROW_TILES, UD], F32, name="o_rows")

        def gate_weight_rows(w):
            return w.rearrange("(u p e) k -> p u e k", u=2, e=2)

        def batch_rows(a):
            return a.rearrange("(p r) k -> p r k", r=ROW_TILES)

        def load_gate_weight(raw, w):
            for u in range(2):
                nc.sync.dma_start(out=raw[:, 2 * u : 2 * u + 2, :], in_=gate_weight_rows(w)[:, u, :, :])

        def load_chunk(j):
            rows = slice(2 * j, 2 * j + 2)
            nc.sync.dma_start(out=hs_raw[:, rows, :], in_=batch_rows(spk_vectors)[:, rows, :])
            nc.sync.dma_start(out=ha_raw[:, rows, :], in_=batch_rows(adr_vectors)[:, rows, :])
            nc.sync.dma_start(out=x_raw[:, rows, :], in_=batch_rows(encoder_hidden)[:, rows, :])

        load_gate_weight(whp_raw, WA_hp)
        load_gate_weight(vhp_raw, VA_hp)
        load_gate_weight(wxp_raw, WA_xp)
        load_chunk(0)
        nc.sync.dma_start(out=vhh_raw[:], in_=VA_hh.rearrange("(j p) k -> p j k", p=P))
        for j in range(1, CHUNKS):
            load_chunk(j)

        nc.vector.memset(warm_in[:], 0.0)
        nc.scalar.activation(out=warm_out[:], in_=warm_in[:], func=SIGMOID)
        make_identity(nc, ident[:])

        copies = []
        waiting = []

        def leave_psum(dst, src):
            if len(copies) % 3 == 2:
                nc.vector.tensor_copy(out=dst, in_=src)
            else:
                nc.scalar.copy(out=dst, in_=src)
            copies.append(1)

        def quantise_waiting(keep_back):
            while len(waiting) > keep_back:
                pairs, codes, scales, plane, cols = waiting.pop(0)
                nc.vector.quantize_mx(
                    out=codes[:, plane, cols].bitcast(FP8X4),
                    scales=scales[:, plane, cols],
                    in_=pairs[:].bitcast(BF16)[:, plane, cols, :].rearrange("p c t -> p (c t)"),
                )

        def to_mx(raw, row, k_pass, pairs, codes, scales, plane, col):
            words = raw[:].bitcast(F32)
            bank = tp_psum.tile([P, 2, CHUNK], F32, name="tp_bank")
            for u in range(2):
                first = 256 * k_pass + P * u
                for i in range(2):
                    nc.tensor.transpose(
                        bank[:, u, P * i : P * i + P], words[:, row + i, first : first + P], ident[:]
                    )
            cols = slice(col, col + CHUNK)
            leave_psum(pairs[:, plane, cols, :], bank[:].rearrange("p u c -> p c u"))
            waiting.append((pairs, codes, scales, plane, cols))
            quantise_waiting(1)

        def weight_to_mx(raw, k_pass, plane):
            for h in range(2):
                to_mx(raw, 2 * h, k_pass, w_pairs, w_codes, w_scales, plane, CHUNK * h)

        weight_to_mx(whp_raw, 0, 0)
        weight_to_mx(vhp_raw, 0, 1)
        weight_to_mx(wxp_raw, 0, 2)
        weight_to_mx(wxp_raw, 1, 3)

        def prepare(j):
            to_mx(hs_raw, 2 * j, 0, a_pairs, a_codes, a_scales, 0, CHUNK * j)
            to_mx(ha_raw, 2 * j, 0, a_pairs, a_codes, a_scales, 1, CHUNK * j)
            to_mx(x_raw, 2 * j, 0, a_pairs, a_codes, a_scales, 2, CHUNK * j)
            to_mx(x_raw, 2 * j, 1, a_pairs, a_codes, a_scales, 3, CHUNK * j)
            if j > 0:
                quantise_waiting(0)

        def gated_state(j):
            cols = slice(CHUNK * j, CHUNK * j + CHUNK)
            for h in range(2):
                sums = gate_psum.tile([P, 2, CHUNK], F32, name="sums")
                for i in range(2):
                    o_cols = slice(P * (2 * h + i), P * (2 * h + i) + P)
                    for s in range(4):
                        nc.tensor.matmul_mx(
                            out=sums[:, i, :],
                            lhsT=w_codes[:, s, o_cols].bitcast(FP8X4),
                            lhsT_scale=w_scales[:, s, o_cols],
                            rhs=a_codes[:, s, cols].bitcast(FP8X4),
                            rhs_scale=a_scales[:, s, cols],
                            start=(s == 0),
                            stop=(s == 3),
                        )
                nc.scalar.activation(out=gate[:, 2 * h : 2 * h + 2, cols], in_=sums[:], func=SIGMOID)
            for r in (2 * j, 2 * j + 1):
                b_cols = slice(P * r, P * r + P)
                nc.vector.tensor_tensor(
                    out=g_vals[:, b_cols, :],
                    in0=gate[:, :, b_cols].rearrange("p t b -> p b t"),
                    in1=a_pairs[:].bitcast(BF16)[:, 1, b_cols, :],
                    op=MULT,
                )
                nc.vector.quantize_mx(
                    out=g_codes[:, b_cols].bitcast(FP8X4),
                    scales=g_scales[:, b_cols],
                    in_=g_vals[:, b_cols, :].rearrange("p c t -> p (c t)"),
                )

        def project(j):
            for r in (2 * j, 2 * j + 1):
                b_cols = slice(P * r, P * r + P)
                proj = out_psum.tile([P, UD], F32, name="proj")
                nc.tensor.matmul_mx(
                    out=proj[:],
                    lhsT=g_codes[:, b_cols].bitcast(FP8X4),
                    lhsT_scale=g_scales[:, b_cols],
                    rhs=w_codes[:, 4, :].bitcast(FP8X4),
                    rhs_scale=w_scales[:, 4, :],
                    start=True,
                    stop=True,
                )
                if r % 2 == 1:
                    nc.vector.tensor_copy(out=o_rows[:, r, :], in_=proj[:])
                else:
                    nc.scalar.copy(out=o_rows[:, r, :], in_=proj[:])
                nc.sync.dma_start(out=batch_rows(out)[:, r : r + 1, :], in_=o_rows[:, r : r + 1, :])

        prepare(0)
        weight_to_mx(vhh_raw, 0, 4)
        quantise_waiting(0)
        for j in range(CHUNKS + 1):
            if j + 1 < CHUNKS:
                prepare(j + 1)
            if j < CHUNKS:
                gated_state(j)
            if j >= 1:
                project(j - 1)
